import numpy as np
import ml_dtypes


def mxq(x, axis, fmt="e4m3"):
    dtype, down = {"e4m3": (ml_dtypes.float8_e4m3fn, 7), "e5m2": (ml_dtypes.float8_e5m2, 14)}[fmt]
    v = np.moveaxis(np.asarray(x, np.float32).astype(ml_dtypes.bfloat16).astype(np.float64), axis, -1)
    blocks = v.reshape(v.shape[:-1] + (-1, 32))
    amax = np.abs(blocks).max(-1, keepdims=True)
    byte = np.maximum(np.where(amax > 0, np.frexp(amax)[1] - 1 + 127, 0) - down, 1)
    scale = np.exp2(byte - 127.0)
    codes = (blocks / scale).astype(np.float32).astype(dtype).astype(np.float64)
    return np.moveaxis((codes * scale).reshape(v.shape), -1, axis)


WIDE = False


def mx_kscale(k):
    if not WIDE:
        return np.ones(k)
    levels = np.array([10, -10, 5, -5, 0])
    if k % 512:
        return np.exp2(np.random.permutation(np.resize(levels, k // 32))).repeat(32)
    a = np.empty((k // 512, 16))
    for p in range(k // 512):
        a[p, :8] = np.random.permutation(np.resize(levels, 8))
        for g in range(8):
            far = levels[np.abs(levels - a[p, g]) >= 10]
            a[p, g + 8] = far[np.random.randint(len(far))]
    return np.exp2(a.ravel()).repeat(32)


BF16 = ml_dtypes.bfloat16


def bf(x):
    return np.asarray(x, np.float32).astype(BF16)


def f64(x):
    return np.asarray(x).astype(np.float64)


E2M1 = np.array([0.0, 0.5, 1.0, 1.5, 2.0, 3.0, 4.0, 6.0, -0.0, -0.5, -1.0, -1.5, -2.0, -3.0, -4.0, -6.0])


def pack_weight(w, fmt):
    k, n = w.shape
    w = f64(bf(w)).reshape(k // 32, 32, n)
    amax = np.abs(w).max(1)
    if fmt == "e4m3":
        byte = np.frexp(amax)[1] - 1 + 127 - 7
    else:
        mant, ex = np.frexp(amax / 6.0)
        byte = np.where(mant > 0.5, ex, ex - 1) + 127
    byte = np.clip(np.where(amax > 0, byte, 1), 1, 254)
    scaled = (w * np.exp2(127.0 - byte)[:, None, :]).reshape(k, n).astype(np.float32)
    by_word = np.ascontiguousarray(scaled.reshape(k // 512, 128, 4, n).transpose(0, 1, 3, 2))
    if fmt == "e4m3":
        words = by_word.astype(ml_dtypes.float8_e4m3fn).view(np.uint8)
    else:
        c = by_word.astype(ml_dtypes.float4_e2m1fn).view(np.uint8) & 0xF
        words = c[..., 0::2] | (c[..., 1::2] << 4)
    return np.ascontiguousarray(words), np.ascontiguousarray(byte.astype(np.uint8).reshape(k // 512, 16, n))


def unpack_weight(words, scales, fmt):
    g, p, n, _ = words.shape
    if fmt == "e4m3":
        vals = np.ascontiguousarray(words).view(ml_dtypes.float8_e4m3fn).astype(np.float64)
    else:
        nib = np.empty((g, p, n, 4), np.uint8)
        nib[..., 0::2] = words & 0xF
        nib[..., 1::2] = words >> 4
        vals = E2M1[nib]
    vals = vals * np.repeat(np.exp2(scales.astype(np.float64) - 127.0), 8, axis=1)[..., None]
    return vals.transpose(0, 1, 3, 2).reshape(g * 512, n)
def pack4(w):
    words, scales = pack_weight(w, "e2m1")
    return words.reshape(words.shape[0], 128, -1), scales


def unpack4(words, scales):
    return unpack_weight(words.reshape(words.shape[0], 128, -1, 2), scales, "e2m1")


B, S, DIM, QL, KVL, H, DN, DR, DV, P0 = 2, 256, 2048, 1536, 512, 16, 128, 128, 128, 37
EPS = 1e-6
HALF = DR // 2


def rms_norm(v, w):
    return v / np.sqrt(np.mean(v * v, axis=-1, keepdims=True) + EPS) * w


def rope(v, start):
    theta = 10000.0 ** (-np.arange(HALF) / HALF)
    pos = np.arange(v.shape[-2]) + start
    ang = pos[:, None] * theta[None, :]
    ang2 = np.concatenate([ang, ang], axis=-1)
    v1, v2 = v[..., :HALF], v[..., HALF:]
    rot = np.concatenate([-v2, v1], axis=-1)
    return v * np.cos(ang2) + rot * np.sin(ang2)


def draw0():
    s, t = mx_kscale(DIM), mx_kscale(QL)
    x = bf(np.random.standard_normal((B, S, DIM)) * s)
    wq_a_words, wq_a_scales = pack4(np.random.standard_normal((DIM, QL)) / np.sqrt(DIM) / s[:, None])
    q_norm_w = bf((1.0 + 0.1 * np.random.standard_normal(QL)) * t)
    wq_b_words, wq_b_scales = pack4(np.random.standard_normal((QL, H * (DN + DR))) / np.sqrt(QL) / t[:, None])
    return {"x": x,
            "wq_a_words": wq_a_words,
            "wq_a_scales": wq_a_scales,
            "q_norm_w": q_norm_w,
            "wq_b_words": wq_b_words,
            "wq_b_scales": wq_b_scales}


def core(x, wq_a_words, wq_a_scales, q_norm_w, wq_b_words, wq_b_scales):
    c = mxq(f64(x), 2, "e4m3") @ unpack4(wq_a_words, wq_a_scales)
    cn = rms_norm(c, f64(q_norm_w))
    q = (mxq(cn, 2, "e4m3") @ unpack4(wq_b_words, wq_b_scales)).reshape(B, S, H, DN + DR)
    q_nope, q_rope = q[..., :DN], q[..., DN:]
    q_rope = rope(q_rope.reshape(B, H, S, DR), P0).reshape(B, S, H, DR)
    return np.concatenate([q_nope, q_rope], axis=-1)


def e4m3fn_bytes(y):
    return np.clip(np.asarray(y, np.float64), -448.0, 448.0).astype(np.float32).astype(ml_dtypes.float8_e4m3fn).view(np.uint8)


def e4m3fn_values(b):
    return np.asarray(b, np.uint8).view(ml_dtypes.float8_e4m3fn).astype(np.float64)


def setup_inputs():
    d = draw0()
    x0 = np.asarray(d['x']).astype(np.float64)
    s = (np.max(np.abs(x0), axis=(0, 1), keepdims=True) / 448.0).astype(np.float32)
    out = {}
    for k, v in d.items():
        if k == 'x':
            out['x_bytes'] = e4m3fn_bytes(x0 / s.astype(np.float64))
            out['x_scale'] = s
        else:
            out[k] = v
    return out


def reference(x_bytes, x_scale, wq_a_words, wq_a_scales, q_norm_w, wq_b_words, wq_b_scales):
    return core(e4m3fn_values(x_bytes) * x_scale.astype(np.float64), wq_a_words, wq_a_scales, q_norm_w, wq_b_words, wq_b_scales)

@@ -1,0 +1,411 @@
+import math
+from contextlib import ExitStack
+
+import concourse.mybir as mybir
+from concourse.masks import make_identity
+
+T, DIM, QL, H, DH = 512, 2048, 1536, 16, 256
+NQ = H * DH
+HALF = 64
+P0 = 37
+EPS = 1e-6
+FLOPS = 2 * T * DIM * QL + 2 * T * QL * NQ
+
+F32 = mybir.dt.float32
+BF16 = mybir.dt.bfloat16
+I32 = mybir.dt.int32
+U32 = mybir.dt.uint32
+U8 = mybir.dt.uint8
+F8 = mybir.dt.float8_e4m3fn
+FP8X4 = mybir.dt.float8_e4m3fn_x4
+FP4X4 = mybir.dt.float4_e2m1fn_x4
+ALU = mybir.AluOpType
+ACT = mybir.ActivationFunctionType
+
+P = 128
+NT = T // P
+GA = DIM // 512
+GB = QL // 512
+NA = QL // 512
+NB = NQ // 512
+
+
+def tile_mla_pa_w4_kernel(tc, x_bytes, x_scale, wq_a_words, wq_a_scales, q_norm_w, wq_b_words, wq_b_scales, out):
+    nc = tc.nc
+    x_rows = x_bytes.rearrange("b s k -> (b s) k")
+    out_rows = out.rearrange("b s h d -> (b s) (h d)")
+
+    with ExitStack() as ctx:
+        keep = ctx.enter_context(tc.tile_pool(name="keep", bufs=1))
+        work = ctx.enter_context(tc.tile_pool(name="work", bufs=3))
+        psum = ctx.enter_context(tc.psum_pool(name="psum", bufs=1))
+        ctx.enter_context(tc.manual_schedule())
+
+        def bank(k):
+            return psum.tile([P, 512], F32, name="bank%d" % k, tag="bank%d" % k)
+
+        def kt(shape, dt, name):
+            return keep.tile(shape, dt, name=name, align_bytes=64)
+
+        xb = [kt([P, DIM], U8, "xb%d" % i) for i in range(NT)]
+        xw = [kt([P, DIM], BF16, "xw%d" % i) for i in range(NT)]
+        xg = [kt([P, GA, 512], BF16, "xg%d" % i) for i in range(NT)]
+        xv = {i: kt([P, GA, 512], BF16, "xv%d" % i) for i in (2, 3)}
+        xq = [kt([P, GA, P], U32, "xq%d" % i) for i in range(NT)]
+        xqs = [kt([P, GA, P], U8, "xqs%d" % i) for i in range(NT)]
+        cn = [kt([P, QL], BF16, "cn%d" % i) for i in range(NT)]
+        cg = [kt([P, GB, 512], BF16, "cg%d" % i) for i in range(NT)]
+        cq = [kt([P, GB, P], U32, "cq%d" % i) for i in range(NT)]
+        cqs = [kt([P, GB, P], U8, "cqs%d" % i) for i in range(NT)]
+        ss = [kt([P, 4], F32, "ss%d" % i) for i in range(NT)]
+        st = [kt([P, 4], F32, "st%d" % i) for i in range(NT)]
+        sd = [kt([P, 4], F32, "sd%d" % i) for i in range(NT)]
+        xs = kt([P, GA, 4], F32, "xs")
+        aw = [kt([P, 2 * QL], U8, "aw%d" % g) for g in range(GA)]
+        asc = kt([P, GA, QL], U8, "asc")
+        bw = [[kt([P, NQ], U8, "bw%d_%d" % (hf, g)) for g in range(GB)] for hf in range(2)]
+        bsc = kt([P, GB, NQ], U8, "bsc")
+        wb = kt([P, QL], BF16, "wb")
+        ident = kt([P, P], F32, "ident")
+        posi = kt([P, H], I32, "posi")
+        posm = kt([P, H], I32, "posm")
+        posf = kt([P, H], F32, "posf")
+        th = kt([P, HALF], F32, "th")
+        ang = kt([P, 2, H, HALF // 2], F32, "ang")
+        rot = kt([P, H, HALF // 2], I32, "rot")
+        half = kt([P, 2, H, HALF // 2], F32, "half")
+        sq = kt([P, 2, H, HALF // 2], F32, "sq")
+        tab = kt([P, 2, H, 2, HALF], F32, "tab")
+        dummy = kt([P, 1], F32, "dummy")
+
+        nc.vector.memset(asc[:].rearrange("p g n -> p (g n)").bitcast(I32), 0)
+        for c in range(2):
+            nc.sync.dma_start(out=xb[0][:, 1024 * c : 1024 * (c + 1)], in_=x_rows[0:P, 1024 * c : 1024 * (c + 1)])
+        nc.sync.dma_start(out=xs[:], in_=x_scale.rearrange("a b (g p t) -> (a b p) g t", p=P, t=4))
+        for q in range(4):
+            nc.sync.dma_start(
+                out=asc[32 * q : 32 * q + 4, :, :].bitcast(I32),
+                in_=wq_a_scales[:, 4 * q : 4 * q + 4, :].rearrange("g r n -> r g n").bitcast(I32),
+            )
+        for g in range(GA):
+            nc.sync.dma_start(out=aw[g][:].bitcast(I32), in_=wq_a_words[g].bitcast(I32))
+            if g == 0:
+                nc.sync.dma_start(out=xb[1][:], in_=x_rows[P : 2 * P, :])
+        nc.sync.dma_start(out=wb[:], in_=q_norm_w.partition_broadcast(P))
+        for i in range(2, NT):
+            nc.sync.dma_start(out=xb[i][:], in_=x_rows[P * i : P * (i + 1), :])
+        nc.gpsimd.iota(posi[:], pattern=[[1, H]], base=0, channel_multiplier=16)
+        make_identity(nc, ident[:])
+
+        nc.vector.memset(th[:, 0:1], 1.0)
+        nc.vector.memset(dummy[:], 0.0)
+        nc.scalar.activation(out=dummy[:], in_=dummy[:], func=ACT.Sin)
+        nc.vector.tensor_scalar(out=th[:, 0:1], in0=th[:, 0:1], scalar1=0.5 / math.pi, scalar2=None, op0=ALU.mult)
+        for w in (1, 4, 16):
+            for m in (1, 2, 3):
+                nc.vector.tensor_scalar(
+                    out=th[:, w * m : w * (m + 1)], in0=th[:, 0:w], scalar1=10000.0 ** (-w * m / 64.0), scalar2=None, op0=ALU.mult
+                )
+        nc.vector.tensor_scalar(out=posm[:], in0=posi[:], scalar1=255, scalar2=None, op0=ALU.bitwise_and)
+        nc.vector.tensor_scalar(out=posf[:], in0=posm[:], scalar1=float(P0), scalar2=None, op0=ALU.add)
+        for eng, a in ((nc.vector, 0), (nc.gpsimd, 1)):
+            eng.tensor_tensor(
+                out=ang[:, a, :, :],
+                in0=posf[:].unsqueeze(2).to_broadcast([P, H, HALF // 2]),
+                in1=th[:, a * (HALF // 2) : (a + 1) * (HALF // 2)].unsqueeze(1).to_broadcast([P, H, HALF // 2]),
+                op=ALU.mult,
+            )
+        nc.gpsimd.memset(bsc[:].rearrange("p g n -> p (g n)").bitcast(I32), 0)
+        for q in range(4):
+            nc.sync.dma_start(
+                out=bsc[32 * q : 32 * q + 4, :, :].bitcast(I32),
+                in_=wq_b_scales[:, 4 * q : 4 * q + 4, :].rearrange("g r n -> r g n").bitcast(I32),
+            )
+        for hf in range(2):
+            for g in range(GB):
+                nc.sync.dma_start(out=bw[hf][g][:].bitcast(I32), in_=wq_b_words[g][:, NQ * hf : NQ * (hf + 1)].bitcast(I32))
+
+        def fold():
+            nc.vector.tensor_copy(out=rot[:], in_=ang[:, 0, :, :])
+            nc.vector.tensor_tensor(out=ang[:, 0, :, :], in0=ang[:, 0, :, :], in1=rot[:], op=ALU.subtract)
+
+        def tables():
+            def col(w, f):
+                return tab[:, w, :, f, :].rearrange("p h (a j) -> p a h j", a=2)
+
+            nc.scalar.activation(out=half[:], in_=ang[:], func=ACT.Sin, scale=math.pi)
+            nc.scalar.activation(out=col(1, 0), in_=ang[:], func=ACT.Sin, scale=2.0 * math.pi)
+            nc.gpsimd.tensor_tensor(out=sq[:], in0=half[:], in1=half[:], op=ALU.mult)
+            for f in range(2):
+                nc.gpsimd.tensor_scalar(out=col(0, f), in0=sq[:], scalar1=-2.0, scalar2=1.0, op0=ALU.mult, op1=ALU.add)
+            nc.gpsimd.tensor_scalar(out=tab[:, 1, :, 1, :], in0=tab[:, 1, :, 0, :], scalar1=1.0, scalar2=0.0, op0=ALU.mult, op1=ALU.add)
+
+        def cast_x(i, c0, c1):
+            nc.scalar.copy(out=xw[i][:, c0:c1], in_=xb[i][:, c0:c1].bitcast(F8))
+
+        def turn_x(i, g, b, slot):
+            words = xw[i][:].bitcast(F32)
+            for u in range(2):
+                o = (2 * slot + u) * P
+                nc.tensor.transpose(b[:, o : o + P], words[:, 256 * g + u : 256 * (g + 1) : 2], ident[:])
+
+        def scale_x(i, g, b, slot):
+            nc.vector.tensor_tensor(
+                out=xg[i][:, g, :].rearrange("p (r u e) -> p r u e", u=2, e=2),
+                in0=b[:, 256 * slot : 256 * (slot + 1)].bitcast(BF16).rearrange("p (u r e) -> p r u e", u=2, e=2),
+                in1=xs[:, g, :].rearrange("p (u e) -> p u e", e=2).unsqueeze(1).to_broadcast([P, P, 2, 2]),
+                op=ALU.mult,
+            )
+
+        def out_x(i, g0, b):
+            nc.scalar.copy(
+                out=xv[i][:, g0 : g0 + 2, :].bitcast(F32).rearrange("p g (r u) -> p g r u", u=2),
+                in_=b[:].rearrange("p (g u r) -> p g r u", u=2, r=P),
+            )
+
+        def gmul_x(i, g0, g1):
+            nc.gpsimd.tensor_tensor(
+                out=xg[i][:, g0:g1, :].rearrange("p g (r t) -> p g r t", t=4),
+                in0=xv[i][:, g0:g1, :].rearrange("p g (r t) -> p g r t", t=4),
+                in1=xs[:, g0:g1, :].unsqueeze(2).to_broadcast([P, g1 - g0, P, 4]),
+                op=ALU.mult,
+            )
+
+        def quant(dst, sc, src, g0, g1):
+            nc.vector.quantize_mx(
+                out=dst[:, g0:g1, :].rearrange("p g c -> p (g c)").bitcast(FP8X4),
+                scales=sc[:, g0:g1, :].rearrange("p g c -> p (g c)"),
+                in_=src[:, g0:g1, :].rearrange("p g c -> p (g c)"),
+            )
+
+        def mm1(i, g, n, b):
+            nc.tensor.matmul_mx(
+                out=b[:],
+                lhsT=xq[i][:, g, :].bitcast(FP8X4),
+                lhsT_scale=xqs[i][:, g, :],
+                rhs=aw[g][:, 1024 * n : 1024 * (n + 1)].bitcast(FP4X4),
+                rhs_scale=asc[:, g, 512 * n : 512 * (n + 1)],
+                start=(g == 0),
+                stop=(g == GA - 1),
+            )
+
+        def square(i, n, b):
+            junk = work.tile([P, 512], BF16, name="junk")
+            nc.scalar.activation(out=junk[:], in_=b[:], func=ACT.Square, accum_out=ss[i][:, n : n + 1])
+
+        def total(i):
+            nc.vector.scalar_tensor_tensor(
+                out=st[i][:, 0:1], in0=ss[i][:, 0:1], scalar=ss[i][:, 1:2], in1=ss[i][:, 2:3], op0=ALU.add, op1=ALU.add
+            )
+            nc.scalar.activation(out=sd[i][:, 0:1], in_=st[i][:, 0:1], func=ACT.Sqrt, scale=1.0 / QL, bias=EPS)
+
+        def invert(i):
+            nc.vector.reciprocal(out=st[i][:, 2:3], in_=sd[i][:, 0:1])
+
+        def apply(i, n, b):
+            nc.vector.scalar_tensor_tensor(
+                out=cn[i][:, 512 * n : 512 * (n + 1)],
+                in0=b[:],
+                scalar=st[i][:, 2:3],
+                in1=wb[:, 512 * n : 512 * (n + 1)],
+                op0=ALU.mult,
+                op1=ALU.mult,
+            )
+
+        def turn_c(i, g, b, slot):
+            words = cn[i][:].bitcast(F32)
+            for u in range(2):
+                o = (2 * slot + u) * P
+                nc.tensor.transpose(b[:, o : o + P], words[:, 256 * g + u : 256 * (g + 1) : 2], ident[:])
+
+        def out_c(i, g0, g1, b):
+            n = g1 - g0
+            nc.scalar.copy(
+                out=cg[i][:, g0:g1, :].bitcast(F32).rearrange("p g (r u) -> p g r u", u=2),
+                in_=b[:, 0 : 256 * n].rearrange("p (g u r) -> p g r u", u=2, r=P),
+            )
+
+        def mm2(i, k, b):
+            for g in range(GB):
+                kk = k % 4
+                nc.tensor.matmul_mx(
+                    out=b[:],
+                    lhsT=cq[i][:, g, :].bitcast(FP8X4),
+                    lhsT_scale=cqs[i][:, g, :],
+                    rhs=bw[k // 4][g][:, 1024 * kk : 1024 * (kk + 1)].bitcast(FP4X4),
+                    rhs_scale=bsc[:, g, 512 * k : 512 * (k + 1)],
+                    start=(g == 0),
+                    stop=(g == GB - 1),
+                )
+
+        state = {}
+
+        def rope(i, k, b):
+            s = k % 2
+            if s == 0:
+                state["res"] = work.tile([P, 4, 2, 2, HALF], F32, name="res", bufs=8)
+                state["t"] = work.tile([P, 2, 4, 2, HALF], F32, name="t", bufs=4)
+            res, t = state["res"], state["t"]
+            v = b[:].rearrange("p (h x c) -> p h x c", h=2, x=2)
+            hs = slice(2 * s, 2 * s + 2)
+            nc.vector.tensor_tensor(
+                out=t[:, :, hs, :, :].rearrange("p w h f j -> p w h (f j)"),
+                in0=v[:, :, 1, :].unsqueeze(1).to_broadcast([P, 2, 2, 2 * HALF]),
+                in1=tab[:, :, 2 * k : 2 * k + 2, :, :].rearrange("p w h f j -> p w h (f j)"),
+                op=ALU.mult,
+            )
+            nc.scalar.copy(out=res[:, hs, 0, :, :].rearrange("p h f j -> p h (f j)"), in_=v[:, :, 0, :])
+            if s == 1:
+                eng = nc.vector if (i == NT - 1 and k == NB - 1) else nc.gpsimd
+                eng.tensor_tensor(out=res[:, :, 1, 0, :], in0=t[:, 0, :, 0, :], in1=t[:, 1, :, 1, :], op=ALU.subtract)
+                eng.tensor_tensor(out=res[:, :, 1, 1, :], in0=t[:, 0, :, 1, :], in1=t[:, 1, :, 0, :], op=ALU.add)
+                nc.sync.dma_start(
+                    out=out_rows[P * i : P * (i + 1), 512 * (k - 1) : 512 * (k + 1)],
+                    in_=res[:].rearrange("p h x f j -> p (h x f j)"),
+                )
+
+        c0 = [bank(n) for n in range(NA)]
+        tb = [bank(3 + g) for g in range(GA)]
+
+        def head_mm(g):
+            for n in range(NA):
+                mm1(0, g, n, c0[n])
+
+        fold()
+        for g in range(GA):
+            cast_x(0, 512 * g, 512 * (g + 1))
+        cast_x(1, 0, 1024)
+        cast_x(1, 1024, 2048)
+        tables()
+        for g in range(GA):
+            turn_x(0, g, tb[g], 0)
+        for g in range(GA):
+            scale_x(0, g, tb[g], 0)
+            quant(xq[0], xqs[0], xg[0], g, g + 1)
+        t1 = [bank(7), bank(3)]
+        head_mm(0)
+        turn_x(1, 0, t1[0], 0)
+        turn_x(1, 1, t1[0], 1)
+        head_mm(1)
+        turn_x(1, 2, t1[1], 0)
+        turn_x(1, 3, t1[1], 1)
+        for n in range(NA):
+            mm1(0, 2, n, c0[n])
+            mm1(0, 3, n, c0[n])
+            square(0, n, c0[n])
+        scale_x(1, 0, t1[0], 0)
+        scale_x(1, 1, t1[0], 1)
+        quant(xq[1], xqs[1], xg[1], 0, 2)
+        scale_x(1, 2, t1[1], 0)
+        scale_x(1, 3, t1[1], 1)
+        quant(xq[1], xqs[1], xg[1], 2, 4)
+        total(0)
+        invert(0)
+        for n in range(NA):
+            apply(0, n, c0[n])
+        c1 = [bank(4 + n) for n in range(NA)]
+        for n in range(NA):
+            mm1(1, 0, n, c1[n])
+            mm1(1, 1, n, c1[n])
+        for n in range(NA):
+            mm1(1, 2, n, c1[n])
+            mm1(1, 3, n, c1[n])
+        tcs = [bank(7), bank(3), bank(0)]
+        square(1, 0, c1[0])
+        for g in range(GB):
+            turn_c(0, g, tcs[g], 0)
+            out_c(0, g, g + 1, tcs[g])
+            quant(cq[0], cqs[0], cg[0], g, g + 1)
+        square(1, 1, c1[1])
+        square(1, 2, c1[2])
+        cast_x(2, 0, 1024)
+
+        cur = {1: c1}
+        ring = [1, 2, 7, 3, 0]
+        cbank = [4, 5, 6]
+        cnt = [0]
+        tx = {}
+        tcb = {}
+        pend = []
+
+        def nextbank():
+            b = bank(ring[cnt[0] % len(ring)])
+            cnt[0] += 1
+            return b
+
+        def do(name, i, a=0):
+            if name == "total":
+                total(i)
+            elif name == "invert":
+                invert(i)
+            elif name == "apply":
+                apply(i, a, cur[i][a])
+            elif name == "cast":
+                cast_x(i, 1024 * a, 1024 * (a + 1))
+            elif name == "turnx":
+                tx[i] = [nextbank(), nextbank()]
+                for g in range(GA):
+                    turn_x(i, g, tx[i][g // 2], g % 2)
+            elif name == "scalex":
+                scale_x(i, a, tx[i][a // 2], a % 2)
+            elif name == "outx":
+                out_x(i, 2 * a, tx[i][a])
+            elif name == "gmul":
+                gmul_x(i, a, a + 1)
+            elif name == "quantx":
+                quant(xq[i], xqs[i], xg[i], 2 * a, 2 * a + 2)
+            elif name == "turnc":
+                tcb[i] = [bank(cbank[1]), bank(cbank[2])]
+                for g in range(GB):
+                    turn_c(i, g, tcb[i][g // 2], g % 2)
+            elif name == "outc":
+                if a == 0:
+                    out_c(i, 0, 2, tcb[i][0])
+                else:
+                    out_c(i, 2, 3, tcb[i][1])
+            elif name == "quantc":
+                if a == 0:
+                    quant(cq[i], cqs[i], cg[i], 0, 2)
+                else:
+                    quant(cq[i], cqs[i], cg[i], 2, 3)
+            elif name == "mm1":
+                b = bank(cbank[a])
+                cur.setdefault(i, []).append(b)
+                for g in range(GA):
+                    mm1(i, g, a, b)
+            elif name == "sq":
+                square(i, a, cur[i][a])
+
+        plan = {
+            (0, 0): [('cast', 2, 1), ('total', 1)],
+            (0, 1): [('invert', 1)],
+            (0, 2): [('turnx', 2), ('scalex', 2, 2), ('outx', 2, 0), ('gmul', 2, 1), ('apply', 1, 1), ('gmul', 2, 0)],
+            (0, 3): [('cast', 3, 1), ('apply', 1, 0), ('apply', 1, 2), ('cast', 3, 0)],
+            (0, 4): [('scalex', 2, 3)],
+            (0, 5): [('quantx', 2, 0), ('turnc', 1), ('outc', 1, 0), ('outc', 1, 1)],
+            (0, 6): [('quantx', 2, 1), ('quantc', 1, 0), ('turnx', 3), ('mm1', 2, 0), ('quantc', 1, 1), ('mm1', 2, 1), ('scalex', 3, 3), ('sq', 2, 0)],
+            (0, 7): [('outx', 3, 0)],
+            (1, 1): [('scalex', 3, 2), ('mm1', 2, 2), ('sq', 2, 1), ('sq', 2, 2), ('gmul', 3, 1)],
+            (1, 2): [('total', 2)],
+            (1, 3): [('invert', 2), ('gmul', 3, 0), ('apply', 2, 1), ('apply', 2, 2), ('apply', 2, 0)],
+            (1, 5): [('quantx', 3, 0), ('turnc', 2), ('outc', 2, 1)],
+            (1, 6): [('outc', 2, 0), ('quantx', 3, 1), ('mm1', 3, 0), ('quantc', 2, 1), ('quantc', 2, 0)],
+            (1, 7): [('mm1', 3, 1)],
+            (2, 0): [('sq', 3, 0), ('mm1', 3, 2), ('sq', 3, 1)],
+            (2, 1): [('sq', 3, 2)],
+            (2, 2): [('total', 3)],
+            (2, 3): [('invert', 3), ('apply', 3, 0), ('apply', 3, 1)],
+            (2, 4): [('apply', 3, 2)],
+            (2, 5): [('turnc', 3), ('outc', 3, 0), ('outc', 3, 1)],
+            (2, 6): [('quantc', 3, 0), ('quantc', 3, 1)],
+        }
+        for i in range(NT):
+            for k in range(NB):
+                b = nextbank()
+                mm2(i, k, b)
+                if pend:
+                    rope(*pend.pop())
+                pend.append((i, k, b))
+                for e in plan.get((i, k), []):
+                    do(*e)
+        rope(*pend.pop())

@@ -23,6 +23,7 @@ ALU = mybir.AluOpType
 ACT = mybir.ActivationFunctionType
 
 P = 128
+WARM = 5
 NT = T // P
 GA = DIM // 512
 GB = QL // 512
@@ -50,7 +51,6 @@ def tile_mla_pa_w4_kernel(tc, x_bytes, x_scale, wq_a_words, wq_a_scales, q_norm_
         xb = [kt([P, DIM], U8, "xb%d" % i) for i in range(NT)]
         xw = [kt([P, DIM], BF16, "xw%d" % i) for i in range(NT)]
         xg = [kt([P, GA, 512], BF16, "xg%d" % i) for i in range(NT)]
-        xv = {i: kt([P, GA, 512], BF16, "xv%d" % i) for i in (2, 3)}
         xq = [kt([P, GA, P], U32, "xq%d" % i) for i in range(NT)]
         xqs = [kt([P, GA, P], U8, "xqs%d" % i) for i in range(NT)]
         cn = [kt([P, QL], BF16, "cn%d" % i) for i in range(NT)]
@@ -66,79 +66,90 @@ def tile_mla_pa_w4_kernel(tc, x_bytes, x_scale, wq_a_words, wq_a_scales, q_norm_
         bw = [[kt([P, NQ], U8, "bw%d_%d" % (hf, g)) for g in range(GB)] for hf in range(2)]
         bsc = kt([P, GB, NQ], U8, "bsc")
         wb = kt([P, QL], BF16, "wb")
+        wrow = kt([P, 512], BF16, "wrow")
+        pick = kt([P, NA], BF16, "pick")
+        zero = kt([P, 512], BF16, "zero")
+        mhalf = kt([P, 1], F32, "mhalf")
         ident = kt([P, P], F32, "ident")
         posi = kt([P, H], I32, "posi")
         posm = kt([P, H], I32, "posm")
         posf = kt([P, H], F32, "posf")
-        th = kt([P, HALF], F32, "th")
+        th = kt([P, HALF // 2], F32, "th")
+        raw = kt([P, H, HALF // 2], F32, "raw")
         ang = kt([P, 2, H, HALF // 2], F32, "ang")
         rot = kt([P, H, HALF // 2], I32, "rot")
-        half = kt([P, 2, H, HALF // 2], F32, "half")
-        sq = kt([P, 2, H, HALF // 2], F32, "sq")
-        tab = kt([P, 2, H, 2, HALF], F32, "tab")
+        aab = kt([P, H, HALF // 2], F32, "aab")
+        ctab = kt([P, H, HALF], F32, "ctab")
+        stab = kt([P, H, HALF], F32, "stab")
         dummy = kt([P, 1], F32, "dummy")
+        one = kt([P, 1], F32, "one")
 
-        nc.vector.memset(asc[:].rearrange("p g n -> p (g n)").bitcast(I32), 0)
-        for c in range(2):
-            nc.sync.dma_start(out=xb[0][:, 1024 * c : 1024 * (c + 1)], in_=x_rows[0:P, 1024 * c : 1024 * (c + 1)])
+        nc.gpsimd.memset(zero[:].bitcast(I32), 0)
+        nc.gpsimd.iota(posi[:], pattern=[[1, H]], base=0, channel_multiplier=16)
+        for k in range(WARM):
+            nc.tensor.matmul(bank(7)[:], zero[:, 0:P], zero[:], start=True, stop=True)
+        nc.vector.memset(one[:], 1.0)
+
+        def zero_asc(h):
+            nc.vector.memset(asc[:, 2 * h : 2 * h + 2, :].rearrange("p g n -> p (g n)").bitcast(I32), 0)
+
+        def zero_bsc(k):
+            nc.vector.memset(bsc[:, k // 2, 2048 * (k % 2) : 2048 * (k % 2 + 1)].bitcast(I32), 0)
+
+        zero_asc(0)
+        nc.vector.tensor_scalar(out=posm[:], in0=posi[:], scalar1=255, scalar2=None, op0=ALU.bitwise_and)
+        nc.vector.tensor_scalar(out=th[:, 0:1], in0=one[:], scalar1=0.5 / math.pi, scalar2=None, op0=ALU.mult)
+        zero_asc(1)
+        for m in (1, 2, 3):
+            nc.vector.tensor_scalar(out=th[:, m : m + 1], in0=th[:, 0:1], scalar1=10000.0 ** (-m / 64.0), scalar2=None, op0=ALU.mult)
+        nc.vector.tensor_scalar(out=posf[:], in0=posm[:], scalar1=float(P0), scalar2=None, op0=ALU.add)
+        zero_bsc(0)
+        for m in (1, 2, 3):
+            nc.vector.tensor_scalar(
+                out=th[:, 4 * m : 4 * m + 4], in0=th[:, 0:4], scalar1=10000.0 ** (-4 * m / 64.0), scalar2=None, op0=ALU.mult
+            )
+        zero_bsc(1)
+        nc.vector.tensor_scalar(out=th[:, 16:32], in0=th[:, 0:16], scalar1=10000.0 ** (-16 / 64.0), scalar2=None, op0=ALU.mult)
+        nc.scalar.activation(out=dummy[:], in_=one[:], func=ACT.Sin)
+        nc.vector.tensor_tensor(
+            out=raw[:],
+            in0=posf[:].unsqueeze(2).to_broadcast([P, H, HALF // 2]),
+            in1=th[:].unsqueeze(1).to_broadcast([P, H, HALF // 2]),
+            op=ALU.mult,
+        )
+
+        nc.sync.dma_start(out=xb[0][:], in_=x_rows[0:P, :])
         nc.sync.dma_start(out=xs[:], in_=x_scale.rearrange("a b (g p t) -> (a b p) g t", p=P, t=4))
         for q in range(4):
             nc.sync.dma_start(
                 out=asc[32 * q : 32 * q + 4, :, :].bitcast(I32),
                 in_=wq_a_scales[:, 4 * q : 4 * q + 4, :].rearrange("g r n -> r g n").bitcast(I32),
             )
-        for g in range(GA):
+        def load_aw(g):
             nc.sync.dma_start(out=aw[g][:].bitcast(I32), in_=wq_a_words[g].bitcast(I32))
-            if g == 0:
-                nc.sync.dma_start(out=xb[1][:], in_=x_rows[P : 2 * P, :])
-        nc.sync.dma_start(out=wb[:], in_=q_norm_w.partition_broadcast(P))
-        for i in range(2, NT):
+
+        def load_x(i):
             nc.sync.dma_start(out=xb[i][:], in_=x_rows[P * i : P * (i + 1), :])
-        nc.gpsimd.iota(posi[:], pattern=[[1, H]], base=0, channel_multiplier=16)
+
+        load_aw(0)
+        load_x(1)
         make_identity(nc, ident[:])
-
-        nc.vector.memset(th[:, 0:1], 1.0)
-        nc.vector.memset(dummy[:], 0.0)
-        nc.scalar.activation(out=dummy[:], in_=dummy[:], func=ACT.Sin)
-        nc.vector.tensor_scalar(out=th[:, 0:1], in0=th[:, 0:1], scalar1=0.5 / math.pi, scalar2=None, op0=ALU.mult)
-        for w in (1, 4, 16):
-            for m in (1, 2, 3):
-                nc.vector.tensor_scalar(
-                    out=th[:, w * m : w * (m + 1)], in0=th[:, 0:w], scalar1=10000.0 ** (-w * m / 64.0), scalar2=None, op0=ALU.mult
-                )
-        nc.vector.tensor_scalar(out=posm[:], in0=posi[:], scalar1=255, scalar2=None, op0=ALU.bitwise_and)
-        nc.vector.tensor_scalar(out=posf[:], in0=posm[:], scalar1=float(P0), scalar2=None, op0=ALU.add)
-        for eng, a in ((nc.vector, 0), (nc.gpsimd, 1)):
-            eng.tensor_tensor(
-                out=ang[:, a, :, :],
-                in0=posf[:].unsqueeze(2).to_broadcast([P, H, HALF // 2]),
-                in1=th[:, a * (HALF // 2) : (a + 1) * (HALF // 2)].unsqueeze(1).to_broadcast([P, H, HALF // 2]),
-                op=ALU.mult,
-            )
-        nc.gpsimd.memset(bsc[:].rearrange("p g n -> p (g n)").bitcast(I32), 0)
-        for q in range(4):
-            nc.sync.dma_start(
-                out=bsc[32 * q : 32 * q + 4, :, :].bitcast(I32),
-                in_=wq_b_scales[:, 4 * q : 4 * q + 4, :].rearrange("g r n -> r g n").bitcast(I32),
-            )
-        for hf in range(2):
-            for g in range(GB):
-                nc.sync.dma_start(out=bw[hf][g][:].bitcast(I32), in_=wq_b_words[g][:, NQ * hf : NQ * (hf + 1)].bitcast(I32))
-
-        def fold():
-            nc.vector.tensor_copy(out=rot[:], in_=ang[:, 0, :, :])
-            nc.vector.tensor_tensor(out=ang[:, 0, :, :], in0=ang[:, 0, :, :], in1=rot[:], op=ALU.subtract)
+        nc.gpsimd.memset(mhalf[:], -0.5)
+        nc.gpsimd.memset(wrow[:].bitcast(I32), 0)
+        nc.gpsimd.tensor_copy(out=pick[:], in_=ident[:, 0:NA])
+        load_aw(1)
+        nc.sync.dma_start(out=wrow[0:NA, :], in_=q_norm_w.rearrange("(r c) -> r c", r=NA))
+        load_aw(2)
+        load_aw(3)
+        load_x(2)
 
         def tables():
-            def col(w, f):
-                return tab[:, w, :, f, :].rearrange("p h (a j) -> p a h j", a=2)
-
-            nc.scalar.activation(out=half[:], in_=ang[:], func=ACT.Sin, scale=math.pi)
-            nc.scalar.activation(out=col(1, 0), in_=ang[:], func=ACT.Sin, scale=2.0 * math.pi)
-            nc.gpsimd.tensor_tensor(out=sq[:], in0=half[:], in1=half[:], op=ALU.mult)
-            for f in range(2):
-                nc.gpsimd.tensor_scalar(out=col(0, f), in0=sq[:], scalar1=-2.0, scalar2=1.0, op0=ALU.mult, op1=ALU.add)
-            nc.gpsimd.tensor_scalar(out=tab[:, 1, :, 1, :], in0=tab[:, 1, :, 0, :], scalar1=1.0, scalar2=0.0, op0=ALU.mult, op1=ALU.add)
+            nc.scalar.activation(out=stab[:].rearrange("p h (a j) -> p a h j", a=2), in_=ang[:], func=ACT.Sin, scale=2.0 * math.pi)
+            nc.scalar.activation(out=aab[:], in_=ang[:, 0, :, :], func=ACT.Abs)
+            for a, src in ((0, aab[:]), (1, ang[:, 1, :, :])):
+                nc.scalar.activation(
+                    out=ctab[:, :, 32 * a : 32 * a + 32], in_=src, func=ACT.Sin, scale=-2.0 * math.pi, bias=0.5 * math.pi
+                )
 
         def cast_x(i, c0, c1):
             nc.scalar.copy(out=xw[i][:, c0:c1], in_=xb[i][:, c0:c1].bitcast(F8))
@@ -154,20 +165,6 @@ def tile_mla_pa_w4_kernel(tc, x_bytes, x_scale, wq_a_words, wq_a_scales, q_norm_
                 out=xg[i][:, g, :].rearrange("p (r u e) -> p r u e", u=2, e=2),
                 in0=b[:, 256 * slot : 256 * (slot + 1)].bitcast(BF16).rearrange("p (u r e) -> p r u e", u=2, e=2),
                 in1=xs[:, g, :].rearrange("p (u e) -> p u e", e=2).unsqueeze(1).to_broadcast([P, P, 2, 2]),
-                op=ALU.mult,
-            )
-
-        def out_x(i, g0, b):
-            nc.scalar.copy(
-                out=xv[i][:, g0 : g0 + 2, :].bitcast(F32).rearrange("p g (r u) -> p g r u", u=2),
-                in_=b[:].rearrange("p (g u r) -> p g r u", u=2, r=P),
-            )
-
-        def gmul_x(i, g0, g1):
-            nc.gpsimd.tensor_tensor(
-                out=xg[i][:, g0:g1, :].rearrange("p g (r t) -> p g r t", t=4),
-                in0=xv[i][:, g0:g1, :].rearrange("p g (r t) -> p g r t", t=4),
-                in1=xs[:, g0:g1, :].unsqueeze(2).to_broadcast([P, g1 - g0, P, 4]),
                 op=ALU.mult,
             )
 
@@ -191,22 +188,20 @@ def tile_mla_pa_w4_kernel(tc, x_bytes, x_scale, wq_a_words, wq_a_scales, q_norm_
 
         def square(i, n, b):
             junk = work.tile([P, 512], BF16, name="junk")
-            nc.scalar.activation(out=junk[:], in_=b[:], func=ACT.Square, accum_out=ss[i][:, n : n + 1])
+            nc.scalar.activation(out=junk[:], in_=b[:], func=ACT.Square, scale=QL ** -0.5, accum_out=ss[i][:, n : n + 1])
 
         def total(i):
             nc.vector.scalar_tensor_tensor(
-                out=st[i][:, 0:1], in0=ss[i][:, 0:1], scalar=ss[i][:, 1:2], in1=ss[i][:, 2:3], op0=ALU.add, op1=ALU.add
+                out=st[i][:, 0:1], in0=ss[i][:, 0:1], scalar=EPS, in1=ss[i][:, 1:2], op0=ALU.add, op1=ALU.add
             )
-            nc.scalar.activation(out=sd[i][:, 0:1], in_=st[i][:, 0:1], func=ACT.Sqrt, scale=1.0 / QL, bias=EPS)
-
-        def invert(i):
-            nc.vector.reciprocal(out=st[i][:, 2:3], in_=sd[i][:, 0:1])
+            nc.vector.tensor_tensor(out=st[i][:, 1:2], in0=st[i][:, 0:1], in1=ss[i][:, 2:3], op=ALU.add)
+            nc.gpsimd.tensor_tensor(out=sd[i][:, 0:1], in0=st[i][:, 1:2], in1=mhalf[:], op=ALU.pow)
 
         def apply(i, n, b):
             nc.vector.scalar_tensor_tensor(
                 out=cn[i][:, 512 * n : 512 * (n + 1)],
                 in0=b[:],
-                scalar=st[i][:, 2:3],
+                scalar=sd[i][:, 0:1],
                 in1=wb[:, 512 * n : 512 * (n + 1)],
                 op0=ALU.mult,
                 op1=ALU.mult,
@@ -248,42 +243,74 @@ def tile_mla_pa_w4_kernel(tc, x_bytes, x_scale, wq_a_words, wq_a_scales, q_norm_
             res, t = state["res"], state["t"]
             v = b[:].rearrange("p (h x c) -> p h x c", h=2, x=2)
             hs = slice(2 * s, 2 * s + 2)
-            nc.vector.tensor_tensor(
-                out=t[:, :, hs, :, :].rearrange("p w h f j -> p w h (f j)"),
-                in0=v[:, :, 1, :].unsqueeze(1).to_broadcast([P, 2, 2, 2 * HALF]),
-                in1=tab[:, :, 2 * k : 2 * k + 2, :, :].rearrange("p w h f j -> p w h (f j)"),
-                op=ALU.mult,
-            )
+            for w, tab in ((0, ctab), (1, stab)):
+                nc.vector.tensor_tensor(
+                    out=t[:, w, hs, :, :],
+                    in0=v[:, :, 1, :].rearrange("p h (f j) -> p h f j", f=2),
+                    in1=tab[:, 2 * k : 2 * k + 2, :].unsqueeze(2).to_broadcast([P, 2, 2, HALF]),
+                    op=ALU.mult,
+                )
             nc.scalar.copy(out=res[:, hs, 0, :, :].rearrange("p h f j -> p h (f j)"), in_=v[:, :, 0, :])
-            if s == 1:
-                eng = nc.vector if (i == NT - 1 and k == NB - 1) else nc.gpsimd
-                eng.tensor_tensor(out=res[:, :, 1, 0, :], in0=t[:, 0, :, 0, :], in1=t[:, 1, :, 1, :], op=ALU.subtract)
-                eng.tensor_tensor(out=res[:, :, 1, 1, :], in0=t[:, 0, :, 1, :], in1=t[:, 1, :, 0, :], op=ALU.add)
+            last = i == NT - 1 and k >= NB - 2
+            if s == 1 or last:
+                hs = slice(2 * s, 2 * s + 2) if last else slice(0, 4)
+                eng = nc.vector if last and s == 1 else nc.gpsimd
+                eng.tensor_tensor(out=res[:, hs, 1, 0, :], in0=t[:, 0, hs, 0, :], in1=t[:, 1, hs, 1, :], op=ALU.subtract)
+                eng.tensor_tensor(out=res[:, hs, 1, 1, :], in0=t[:, 0, hs, 1, :], in1=t[:, 1, hs, 0, :], op=ALU.add)
+                n0 = 512 * k if last else 512 * (k - 1)
                 nc.sync.dma_start(
-                    out=out_rows[P * i : P * (i + 1), 512 * (k - 1) : 512 * (k + 1)],
-                    in_=res[:].rearrange("p h x f j -> p (h x f j)"),
+                    out=out_rows[P * i : P * (i + 1), n0 : 512 * (k + 1)],
+                    in_=res[:, hs, :, :, :].rearrange("p h x f j -> p (h x f j)"),
                 )
 
         c0 = [bank(n) for n in range(NA)]
         tb = [bank(3 + g) for g in range(GA)]
 
+        def spread_w(n, b, half):
+            nc.tensor.matmul(
+                b[:].bitcast(BF16)[:, 512 * half : 512 * (half + 1)], pick[:, n : n + 1].to_broadcast([P, P]), wrow[:], start=True, stop=True
+            )
+
         def head_mm(g):
             for n in range(NA):
                 mm1(0, g, n, c0[n])
 
-        fold()
         for g in range(GA):
             cast_x(0, 512 * g, 512 * (g + 1))
         cast_x(1, 0, 1024)
         cast_x(1, 1024, 2048)
-        tables()
         for g in range(GA):
             turn_x(0, g, tb[g], 0)
         for g in range(GA):
             scale_x(0, g, tb[g], 0)
-            quant(xq[0], xqs[0], xg[0], g, g + 1)
-        t1 = [bank(7), bank(3)]
+            if g > 0:
+                quant(xq[0], xqs[0], xg[0], g - 1, g)
+        nc.vector.tensor_copy(out=rot[:], in_=raw[:])
+        quant(xq[0], xqs[0], xg[0], 3, 4)
+        nc.vector.tensor_scalar(out=ang[:, 1, :, :], in0=raw[:], scalar1=0.01, scalar2=None, op0=ALU.mult)
+        nc.vector.tensor_tensor(out=ang[:, 0, :, :], in0=raw[:], in1=rot[:], op=ALU.subtract)
+        zero_bsc(2)
+        zero_bsc(3)
+        zero_bsc(4)
+        zero_bsc(5)
+        for q in range(4):
+            nc.sync.dma_start(
+                out=bsc[32 * q : 32 * q + 4, :, :].bitcast(I32),
+                in_=wq_b_scales[:, 4 * q : 4 * q + 4, :].rearrange("g r n -> r g n").bitcast(I32),
+            )
+        for hf in range(2):
+            for g in range(GB):
+                nc.sync.dma_start(out=bw[hf][g][:].bitcast(I32), in_=wq_b_words[g][:, NQ * hf : NQ * (hf + 1)].bitcast(I32))
+            if hf == 0:
+                load_x(3)
+        tables()
+        t1 = [bank(4), bank(5)]
         head_mm(0)
+        wa = bank(7)
+        wc = bank(3)
+        spread_w(0, wa, 0)
+        spread_w(1, wa, 1)
+        spread_w(2, wc, 0)
         turn_x(1, 0, t1[0], 0)
         turn_x(1, 1, t1[0], 1)
         head_mm(1)
@@ -293,36 +320,35 @@ def tile_mla_pa_w4_kernel(tc, x_bytes, x_scale, wq_a_words, wq_a_scales, q_norm_
             mm1(0, 2, n, c0[n])
             mm1(0, 3, n, c0[n])
             square(0, n, c0[n])
-        scale_x(1, 0, t1[0], 0)
-        scale_x(1, 1, t1[0], 1)
-        quant(xq[1], xqs[1], xg[1], 0, 2)
-        scale_x(1, 2, t1[1], 0)
-        scale_x(1, 3, t1[1], 1)
+        for g in range(GA):
+            scale_x(1, g, t1[g // 2], g % 2)
+            if g == 2:
+                quant(xq[1], xqs[1], xg[1], 0, 2)
         quant(xq[1], xqs[1], xg[1], 2, 4)
+        nc.vector.tensor_copy(out=wb[:, 0:1024], in_=wa[:].bitcast(BF16))
+        nc.scalar.copy(out=wb[:, 1024:1536], in_=wc[:, 0:256].bitcast(BF16))
         total(0)
-        invert(0)
+        cast_x(2, 0, 1024)
         for n in range(NA):
             apply(0, n, c0[n])
-        c1 = [bank(4 + n) for n in range(NA)]
+        c1 = [bank((6, 4, 5)[n]) for n in range(NA)]
         for n in range(NA):
             mm1(1, 0, n, c1[n])
             mm1(1, 1, n, c1[n])
         for n in range(NA):
             mm1(1, 2, n, c1[n])
             mm1(1, 3, n, c1[n])
-        tcs = [bank(7), bank(3), bank(0)]
-        square(1, 0, c1[0])
+        tcs = [bank(0), bank(7), bank(3)]
         for g in range(GB):
             turn_c(0, g, tcs[g], 0)
             out_c(0, g, g + 1, tcs[g])
             quant(cq[0], cqs[0], cg[0], g, g + 1)
-        square(1, 1, c1[1])
-        square(1, 2, c1[2])
-        cast_x(2, 0, 1024)
+        for n in range(NA):
+            square(1, n, c1[n])
 
         cur = {1: c1}
-        ring = [1, 2, 7, 3, 0]
-        cbank = [4, 5, 6]
+        ring = [1, 2, 0, 7, 3]
+        cbank = [6, 4, 5]
         cnt = [0]
         tx = {}
         tcb = {}
@@ -336,8 +362,6 @@ def tile_mla_pa_w4_kernel(tc, x_bytes, x_scale, wq_a_words, wq_a_scales, q_norm_
         def do(name, i, a=0):
             if name == "total":
                 total(i)
-            elif name == "invert":
-                invert(i)
             elif name == "apply":
                 apply(i, a, cur[i][a])
             elif name == "cast":
@@ -348,10 +372,6 @@ def tile_mla_pa_w4_kernel(tc, x_bytes, x_scale, wq_a_words, wq_a_scales, q_norm_
                     turn_x(i, g, tx[i][g // 2], g % 2)
             elif name == "scalex":
                 scale_x(i, a, tx[i][a // 2], a % 2)
-            elif name == "outx":
-                out_x(i, 2 * a, tx[i][a])
-            elif name == "gmul":
-                gmul_x(i, a, a + 1)
             elif name == "quantx":
                 quant(xq[i], xqs[i], xg[i], 2 * a, 2 * a + 2)
             elif name == "turnc":
@@ -377,26 +397,22 @@ def tile_mla_pa_w4_kernel(tc, x_bytes, x_scale, wq_a_words, wq_a_scales, q_norm_
                 square(i, a, cur[i][a])
 
         plan = {
-            (0, 0): [('cast', 2, 1), ('total', 1)],
-            (0, 1): [('invert', 1)],
-            (0, 2): [('turnx', 2), ('scalex', 2, 2), ('outx', 2, 0), ('gmul', 2, 1), ('apply', 1, 1), ('gmul', 2, 0)],
-            (0, 3): [('cast', 3, 1), ('apply', 1, 0), ('apply', 1, 2), ('cast', 3, 0)],
-            (0, 4): [('scalex', 2, 3)],
-            (0, 5): [('quantx', 2, 0), ('turnc', 1), ('outc', 1, 0), ('outc', 1, 1)],
-            (0, 6): [('quantx', 2, 1), ('quantc', 1, 0), ('turnx', 3), ('mm1', 2, 0), ('quantc', 1, 1), ('mm1', 2, 1), ('scalex', 3, 3), ('sq', 2, 0)],
-            (0, 7): [('outx', 3, 0)],
-            (1, 1): [('scalex', 3, 2), ('mm1', 2, 2), ('sq', 2, 1), ('sq', 2, 2), ('gmul', 3, 1)],
-            (1, 2): [('total', 2)],
-            (1, 3): [('invert', 2), ('gmul', 3, 0), ('apply', 2, 1), ('apply', 2, 2), ('apply', 2, 0)],
-            (1, 5): [('quantx', 3, 0), ('turnc', 2), ('outc', 2, 1)],
-            (1, 6): [('outc', 2, 0), ('quantx', 3, 1), ('mm1', 3, 0), ('quantc', 2, 1), ('quantc', 2, 0)],
-            (1, 7): [('mm1', 3, 1)],
-            (2, 0): [('sq', 3, 0), ('mm1', 3, 2), ('sq', 3, 1)],
-            (2, 1): [('sq', 3, 2)],
-            (2, 2): [('total', 3)],
-            (2, 3): [('invert', 3), ('apply', 3, 0), ('apply', 3, 1)],
-            (2, 4): [('apply', 3, 2)],
-            (2, 5): [('turnc', 3), ('outc', 3, 0), ('outc', 3, 1)],
+            (0, 1): [('cast', 2, 1), ('total', 1)],
+            (0, 3): [('cast', 3, 0), ('apply', 1, 2)],
+            (0, 4): [('apply', 1, 1), ('turnx', 2), ('apply', 1, 0)],
+            (0, 5): [('scalex', 2, 2), ('turnc', 1), ('scalex', 2, 0), ('scalex', 2, 1), ('cast', 3, 1), ('scalex', 2, 3), ('outc', 1, 0)],
+            (0, 6): [('turnx', 3), ('quantc', 1, 0), ('outc', 1, 1), ('quantx', 2, 0), ('quantx', 2, 1)],
+            (0, 7): [('mm1', 2, 0), ('scalex', 3, 3), ('sq', 2, 0), ('quantc', 1, 1), ('scalex', 3, 0), ('mm1', 2, 1), ('scalex', 3, 1)],
+            (1, 2): [('mm1', 2, 2), ('sq', 2, 1), ('sq', 2, 2), ('scalex', 3, 2), ('quantx', 3, 0)],
+            (1, 3): [('total', 2)],
+            (1, 4): [('apply', 2, 0), ('apply', 2, 1), ('apply', 2, 2)],
+            (1, 5): [('turnc', 2), ('quantx', 3, 1), ('outc', 2, 0)],
+            (1, 6): [('outc', 2, 1), ('mm1', 3, 0), ('quantc', 2, 1), ('mm1', 3, 1), ('mm1', 3, 2), ('quantc', 2, 0), ('sq', 3, 0), ('sq', 3, 1), ('sq', 3, 2)],
+            (1, 7): [('total', 3)],
+            (2, 0): [('apply', 3, 2)],
+            (2, 1): [('apply', 3, 1), ('apply', 3, 0)],
+            (2, 4): [('turnc', 3), ('outc', 3, 0)],
+            (2, 5): [('outc', 3, 1)],
             (2, 6): [('quantc', 3, 0), ('quantc', 3, 1)],
         }
         for i in range(NT):

@@ -46,7 +46,7 @@ def tile_mla_pa_w4_kernel(tc, x_bytes, x_scale, wq_a_words, wq_a_scales, q_norm_
             return psum.tile([P, 512], F32, name="bank%d" % k, tag="bank%d" % k)
 
         def kt(shape, dt, name):
-            return keep.tile(shape, dt, name=name, align_bytes=64)
+            return keep.tile(shape, dt, name=name, align_bytes=256 if shape[-1] >= 128 else 64)
 
         xb = [kt([P, DIM], U8, "xb%d" % i) for i in range(NT)]
         xw = [kt([P, DIM], BF16, "xw%d" % i) for i in range(NT)]
@@ -79,8 +79,7 @@ def tile_mla_pa_w4_kernel(tc, x_bytes, x_scale, wq_a_words, wq_a_scales, q_norm_
         ang = kt([P, 2, H, HALF // 2], F32, "ang")
         rot = kt([P, H, HALF // 2], I32, "rot")
         aab = kt([P, H, HALF // 2], F32, "aab")
-        ctab = kt([P, H, HALF], F32, "ctab")
-        stab = kt([P, H, HALF], F32, "stab")
+        tab = kt([P, 2, H, 2, HALF], F32, "tab")
         dummy = kt([P, 1], F32, "dummy")
         one = kt([P, 1], F32, "one")
 
@@ -118,38 +117,43 @@ def tile_mla_pa_w4_kernel(tc, x_bytes, x_scale, wq_a_words, wq_a_scales, q_norm_
             op=ALU.mult,
         )
 
-        nc.sync.dma_start(out=xb[0][:], in_=x_rows[0:P, :])
-        nc.sync.dma_start(out=xs[:], in_=x_scale.rearrange("a b (g p t) -> (a b p) g t", p=P, t=4))
-        for q in range(4):
-            nc.sync.dma_start(
-                out=asc[32 * q : 32 * q + 4, :, :].bitcast(I32),
-                in_=wq_a_scales[:, 4 * q : 4 * q + 4, :].rearrange("g r n -> r g n").bitcast(I32),
-            )
         def load_aw(g):
             nc.sync.dma_start(out=aw[g][:].bitcast(I32), in_=wq_a_words[g].bitcast(I32))
 
         def load_x(i):
             nc.sync.dma_start(out=xb[i][:], in_=x_rows[P * i : P * (i + 1), :])
 
+        load_x(0)
         load_aw(0)
+        nc.sync.dma_start(out=xs[:], in_=x_scale.rearrange("a b (g p t) -> (a b p) g t", p=P, t=4))
         load_x(1)
+        for q in range(4):
+            nc.sync.dma_start(
+                out=asc[32 * q : 32 * q + 4, :, :].bitcast(I32),
+                in_=wq_a_scales[:, 4 * q : 4 * q + 4, :].rearrange("g r n -> r g n").bitcast(I32),
+            )
         make_identity(nc, ident[:])
         nc.gpsimd.memset(mhalf[:], -0.5)
         nc.gpsimd.memset(wrow[:].bitcast(I32), 0)
         nc.gpsimd.tensor_copy(out=pick[:], in_=ident[:, 0:NA])
         load_aw(1)
-        nc.sync.dma_start(out=wrow[0:NA, :], in_=q_norm_w.rearrange("(r c) -> r c", r=NA))
         load_aw(2)
+        nc.sync.dma_start(out=wrow[0:NA, :], in_=q_norm_w.rearrange("(r c) -> r c", r=NA))
         load_aw(3)
         load_x(2)
 
         def tables():
-            nc.scalar.activation(out=stab[:].rearrange("p h (a j) -> p a h j", a=2), in_=ang[:], func=ACT.Sin, scale=2.0 * math.pi)
+            nc.scalar.activation(
+                out=tab[:, 1, :, 0, :].rearrange("p h (a j) -> p a h j", a=2), in_=ang[:], func=ACT.Sin, scale=2.0 * math.pi
+            )
             nc.scalar.activation(out=aab[:], in_=ang[:, 0, :, :], func=ACT.Abs)
             for a, src in ((0, aab[:]), (1, ang[:, 1, :, :])):
                 nc.scalar.activation(
-                    out=ctab[:, :, 32 * a : 32 * a + 32], in_=src, func=ACT.Sin, scale=-2.0 * math.pi, bias=0.5 * math.pi
+                    out=tab[:, 0, :, 0, 32 * a : 32 * a + 32], in_=src, func=ACT.Sin, scale=-2.0 * math.pi, bias=0.5 * math.pi
                 )
+
+        def twin(w):
+            nc.gpsimd.tensor_scalar(out=tab[:, w, :, 1, :], in0=tab[:, w, :, 0, :], scalar1=1.0, scalar2=0.0, op0=ALU.mult, op1=ALU.add)
 
         def cast_x(i, c0, c1):
             nc.scalar.copy(out=xw[i][:, c0:c1], in_=xb[i][:, c0:c1].bitcast(F8))
@@ -239,24 +243,23 @@ def tile_mla_pa_w4_kernel(tc, x_bytes, x_scale, wq_a_words, wq_a_scales, q_norm_
             s = k % 2
             if s == 0:
                 state["res"] = work.tile([P, 4, 2, 2, HALF], F32, name="res", bufs=8)
-                state["t"] = work.tile([P, 2, 4, 2, HALF], F32, name="t", bufs=4)
+                state["t"] = work.tile([P, 4, 2, 2, HALF], F32, name="t", bufs=4)
             res, t = state["res"], state["t"]
             v = b[:].rearrange("p (h x c) -> p h x c", h=2, x=2)
             hs = slice(2 * s, 2 * s + 2)
-            for w, tab in ((0, ctab), (1, stab)):
-                nc.vector.tensor_tensor(
-                    out=t[:, w, hs, :, :],
-                    in0=v[:, :, 1, :].rearrange("p h (f j) -> p h f j", f=2),
-                    in1=tab[:, 2 * k : 2 * k + 2, :].unsqueeze(2).to_broadcast([P, 2, 2, HALF]),
-                    op=ALU.mult,
-                )
+            nc.vector.tensor_tensor(
+                out=t[:, hs, :, :, :].rearrange("p h w f j -> p w h (f j)"),
+                in0=v[:, :, 1, :].unsqueeze(1).to_broadcast([P, 2, 2, 2 * HALF]),
+                in1=tab[:, :, 2 * k : 2 * k + 2, :, :].rearrange("p w h f j -> p w h (f j)"),
+                op=ALU.mult,
+            )
             nc.scalar.copy(out=res[:, hs, 0, :, :].rearrange("p h f j -> p h (f j)"), in_=v[:, :, 0, :])
             last = i == NT - 1 and k >= NB - 2
             if s == 1 or last:
                 hs = slice(2 * s, 2 * s + 2) if last else slice(0, 4)
                 eng = nc.vector if last and s == 1 else nc.gpsimd
-                eng.tensor_tensor(out=res[:, hs, 1, 0, :], in0=t[:, 0, hs, 0, :], in1=t[:, 1, hs, 1, :], op=ALU.subtract)
-                eng.tensor_tensor(out=res[:, hs, 1, 1, :], in0=t[:, 0, hs, 1, :], in1=t[:, 1, hs, 0, :], op=ALU.add)
+                eng.tensor_tensor(out=res[:, hs, 1, 0, :], in0=t[:, hs, 0, 0, :], in1=t[:, hs, 1, 1, :], op=ALU.subtract)
+                eng.tensor_tensor(out=res[:, hs, 1, 1, :], in0=t[:, hs, 0, 1, :], in1=t[:, hs, 1, 0, :], op=ALU.add)
                 n0 = 512 * k if last else 512 * (k - 1)
                 nc.sync.dma_start(
                     out=out_rows[P * i : P * (i + 1), n0 : 512 * (k + 1)],
@@ -304,6 +307,7 @@ def tile_mla_pa_w4_kernel(tc, x_bytes, x_scale, wq_a_words, wq_a_scales, q_norm_
             if hf == 0:
                 load_x(3)
         tables()
+        twin(1)
         t1 = [bank(4), bank(5)]
         head_mm(0)
         wa = bank(7)
@@ -311,11 +315,9 @@ def tile_mla_pa_w4_kernel(tc, x_bytes, x_scale, wq_a_words, wq_a_scales, q_norm_
         spread_w(0, wa, 0)
         spread_w(1, wa, 1)
         spread_w(2, wc, 0)
-        turn_x(1, 0, t1[0], 0)
-        turn_x(1, 1, t1[0], 1)
         head_mm(1)
-        turn_x(1, 2, t1[1], 0)
-        turn_x(1, 3, t1[1], 1)
+        for g in range(GA):
+            turn_x(1, g, t1[g // 2], g % 2)
         for n in range(NA):
             mm1(0, 2, n, c0[n])
             mm1(0, 3, n, c0[n])
@@ -328,6 +330,7 @@ def tile_mla_pa_w4_kernel(tc, x_bytes, x_scale, wq_a_words, wq_a_scales, q_norm_
         nc.vector.tensor_copy(out=wb[:, 0:1024], in_=wa[:].bitcast(BF16))
         nc.scalar.copy(out=wb[:, 1024:1536], in_=wc[:, 0:256].bitcast(BF16))
         total(0)
+        twin(0)
         cast_x(2, 0, 1024)
         for n in range(NA):
             apply(0, n, c0[n])
@@ -397,23 +400,25 @@ def tile_mla_pa_w4_kernel(tc, x_bytes, x_scale, wq_a_words, wq_a_scales, q_norm_
                 square(i, a, cur[i][a])
 
         plan = {
-            (0, 1): [('cast', 2, 1), ('total', 1)],
-            (0, 3): [('cast', 3, 0), ('apply', 1, 2)],
-            (0, 4): [('apply', 1, 1), ('turnx', 2), ('apply', 1, 0)],
-            (0, 5): [('scalex', 2, 2), ('turnc', 1), ('scalex', 2, 0), ('scalex', 2, 1), ('cast', 3, 1), ('scalex', 2, 3), ('outc', 1, 0)],
-            (0, 6): [('turnx', 3), ('quantc', 1, 0), ('outc', 1, 1), ('quantx', 2, 0), ('quantx', 2, 1)],
-            (0, 7): [('mm1', 2, 0), ('scalex', 3, 3), ('sq', 2, 0), ('quantc', 1, 1), ('scalex', 3, 0), ('mm1', 2, 1), ('scalex', 3, 1)],
-            (1, 2): [('mm1', 2, 2), ('sq', 2, 1), ('sq', 2, 2), ('scalex', 3, 2), ('quantx', 3, 0)],
-            (1, 3): [('total', 2)],
-            (1, 4): [('apply', 2, 0), ('apply', 2, 1), ('apply', 2, 2)],
-            (1, 5): [('turnc', 2), ('quantx', 3, 1), ('outc', 2, 0)],
-            (1, 6): [('outc', 2, 1), ('mm1', 3, 0), ('quantc', 2, 1), ('mm1', 3, 1), ('mm1', 3, 2), ('quantc', 2, 0), ('sq', 3, 0), ('sq', 3, 1), ('sq', 3, 2)],
-            (1, 7): [('total', 3)],
-            (2, 0): [('apply', 3, 2)],
-            (2, 1): [('apply', 3, 1), ('apply', 3, 0)],
-            (2, 4): [('turnc', 3), ('outc', 3, 0)],
-            (2, 5): [('outc', 3, 1)],
-            (2, 6): [('quantc', 3, 0), ('quantc', 3, 1)],
+            (0, 0): [('cast', 2, 1)],
+            (0, 1): [('total', 1)],
+            (0, 3): [('apply', 1, 1)],
+            (0, 4): [('cast', 3, 0)],
+            (0, 5): [('apply', 1, 0), ('turnx', 2)],
+            (0, 6): [('apply', 1, 2), ('scalex', 2, 3), ('scalex', 2, 0), ('scalex', 2, 2), ('scalex', 2, 1), ('cast', 3, 1), ('turnc', 1), ('outc', 1, 1), ('outc', 1, 0), ('quantx', 2, 1), ('quantx', 2, 0), ('turnx', 3)],
+            (0, 7): [('mm1', 2, 0), ('mm1', 2, 1), ('quantc', 1, 0), ('quantc', 1, 1), ('mm1', 2, 2), ('scalex', 3, 3), ('scalex', 3, 2), ('scalex', 3, 1), ('sq', 2, 1), ('sq', 2, 0)],
+            (1, 0): [('quantx', 3, 1), ('sq', 2, 2), ('scalex', 3, 0)],
+            (1, 1): [('total', 2)],
+            (1, 2): [('apply', 2, 0)],
+            (1, 3): [('quantx', 3, 0), ('apply', 2, 1), ('apply', 2, 2)],
+            (1, 5): [('turnc', 2), ('outc', 2, 0), ('outc', 2, 1), ('mm1', 3, 0)],
+            (1, 6): [('quantc', 2, 1), ('quantc', 2, 0), ('sq', 3, 0), ('mm1', 3, 1), ('mm1', 3, 2), ('sq', 3, 1)],
+            (1, 7): [('sq', 3, 2), ('total', 3)],
+            (2, 0): [('apply', 3, 0)],
+            (2, 3): [('apply', 3, 1), ('apply', 3, 2)],
+            (2, 4): [('turnc', 3), ('outc', 3, 1), ('outc', 3, 0)],
+            (2, 6): [('quantc', 3, 0)],
+            (2, 7): [('quantc', 3, 1)],
         }
         for i in range(NT):
             for k in range(NB):

@@ -64,7 +64,7 @@ def tile_mla_pa_w4_kernel(tc, x_bytes, x_scale, wq_a_words, wq_a_scales, q_norm_
         aw = [kt([P, 2 * QL], U8, "aw%d" % g) for g in range(GA)]
         asc = kt([P, GA, QL], U8, "asc")
         bw = [[kt([P, NQ], U8, "bw%d_%d" % (hf, g)) for g in range(GB)] for hf in range(2)]
-        bsc = kt([P, GB, NQ], U8, "bsc")
+        bsc = [kt([P, GB, NQ // 2], U8, "bsc%d" % h) for h in range(2)]
         wb = kt([P, QL], BF16, "wb")
         wrow = kt([P, 512], BF16, "wrow")
         pick = kt([P, NA], BF16, "pick")
@@ -89,26 +89,65 @@ def tile_mla_pa_w4_kernel(tc, x_bytes, x_scale, wq_a_words, wq_a_scales, q_norm_
             nc.tensor.matmul(bank(7)[:], zero[:, 0:P], zero[:], start=True, stop=True)
         nc.vector.memset(one[:], 1.0)
 
-        def zero_asc(h):
-            nc.vector.memset(asc[:, 2 * h : 2 * h + 2, :].rearrange("p g n -> p (g n)").bitcast(I32), 0)
+        def zero_asc(g0, g1):
+            nc.vector.memset(asc[:, g0:g1, :].rearrange("p g n -> p (g n)").bitcast(I32), 0)
 
-        def zero_bsc(k):
-            nc.vector.memset(bsc[:, k // 2, 2048 * (k % 2) : 2048 * (k % 2 + 1)].bitcast(I32), 0)
+        def zero_bsc(h, g):
+            nc.vector.memset(bsc[h][:, g, :].bitcast(I32), 0)
 
-        zero_asc(0)
+        def load_asc(g0, g1):
+            for q in range(4):
+                nc.sync.dma_start(
+                    out=asc[32 * q : 32 * q + 4, g0:g1, :].bitcast(I32),
+                    in_=wq_a_scales[g0:g1, 4 * q : 4 * q + 4, :].rearrange("g r n -> r g n").bitcast(I32),
+                )
+
+        def load_bsc(h):
+            for q in range(4):
+                nc.sync.dma_start(
+                    out=bsc[h][32 * q : 32 * q + 4, :, :].bitcast(I32),
+                    in_=wq_b_scales[:, 4 * q : 4 * q + 4, 2048 * h : 2048 * (h + 1)].rearrange("g r n -> r g n").bitcast(I32),
+                )
+
+        def load_aw(g):
+            nc.sync.dma_start(out=aw[g][:].bitcast(I32), in_=wq_a_words[g].bitcast(I32))
+
+        def load_bw(h):
+            for g in range(GB):
+                nc.sync.dma_start(out=bw[h][g][:].bitcast(I32), in_=wq_b_words[g][:, NQ * h : NQ * (h + 1)].bitcast(I32))
+
+        def load_x(i):
+            nc.sync.dma_start(out=xb[i][:], in_=x_rows[P * i : P * (i + 1), :])
+
+        nc.gpsimd.memset(wrow[:].bitcast(I32), 0)
+        zero_asc(0, 2)
+        load_x(0)
+        load_asc(0, 2)
+        load_aw(0)
+        nc.sync.dma_start(out=xs[:], in_=x_scale.rearrange("a b (g p t) -> (a b p) g t", p=P, t=4))
+        nc.sync.dma_start(out=wrow[0:NA, :], in_=q_norm_w.rearrange("(r c) -> r c", r=NA))
+        load_aw(1)
+        load_x(1)
         nc.vector.tensor_scalar(out=posm[:], in0=posi[:], scalar1=255, scalar2=None, op0=ALU.bitwise_and)
         nc.vector.tensor_scalar(out=th[:, 0:1], in0=one[:], scalar1=0.5 / math.pi, scalar2=None, op0=ALU.mult)
-        zero_asc(1)
+        zero_asc(2, 4)
+        load_asc(2, 4)
+        load_aw(2)
+        load_aw(3)
         for m in (1, 2, 3):
             nc.vector.tensor_scalar(out=th[:, m : m + 1], in0=th[:, 0:1], scalar1=10000.0 ** (-m / 64.0), scalar2=None, op0=ALU.mult)
         nc.vector.tensor_scalar(out=posf[:], in0=posm[:], scalar1=float(P0), scalar2=None, op0=ALU.add)
-        zero_bsc(0)
+        zero_bsc(0, 0)
         for m in (1, 2, 3):
             nc.vector.tensor_scalar(
                 out=th[:, 4 * m : 4 * m + 4], in0=th[:, 0:4], scalar1=10000.0 ** (-4 * m / 64.0), scalar2=None, op0=ALU.mult
             )
-        zero_bsc(1)
+        zero_bsc(0, 1)
         nc.vector.tensor_scalar(out=th[:, 16:32], in0=th[:, 0:16], scalar1=10000.0 ** (-16 / 64.0), scalar2=None, op0=ALU.mult)
+        zero_bsc(0, 2)
+        load_bsc(0)
+        load_x(2)
+        load_bw(0)
         nc.scalar.activation(out=dummy[:], in_=one[:], func=ACT.Sin)
         nc.vector.tensor_tensor(
             out=raw[:],
@@ -116,31 +155,9 @@ def tile_mla_pa_w4_kernel(tc, x_bytes, x_scale, wq_a_words, wq_a_scales, q_norm_
             in1=th[:].unsqueeze(1).to_broadcast([P, H, HALF // 2]),
             op=ALU.mult,
         )
-
-        def load_aw(g):
-            nc.sync.dma_start(out=aw[g][:].bitcast(I32), in_=wq_a_words[g].bitcast(I32))
-
-        def load_x(i):
-            nc.sync.dma_start(out=xb[i][:], in_=x_rows[P * i : P * (i + 1), :])
-
-        load_x(0)
-        load_aw(0)
-        nc.sync.dma_start(out=xs[:], in_=x_scale.rearrange("a b (g p t) -> (a b p) g t", p=P, t=4))
-        load_x(1)
-        for q in range(4):
-            nc.sync.dma_start(
-                out=asc[32 * q : 32 * q + 4, :, :].bitcast(I32),
-                in_=wq_a_scales[:, 4 * q : 4 * q + 4, :].rearrange("g r n -> r g n").bitcast(I32),
-            )
         make_identity(nc, ident[:])
         nc.gpsimd.memset(mhalf[:], -0.5)
-        nc.gpsimd.memset(wrow[:].bitcast(I32), 0)
         nc.gpsimd.tensor_copy(out=pick[:], in_=ident[:, 0:NA])
-        load_aw(1)
-        load_aw(2)
-        nc.sync.dma_start(out=wrow[0:NA, :], in_=q_norm_w.rearrange("(r c) -> r c", r=NA))
-        load_aw(3)
-        load_x(2)
 
         def tables():
             nc.scalar.activation(
@@ -202,20 +219,22 @@ def tile_mla_pa_w4_kernel(tc, x_bytes, x_scale, wq_a_words, wq_a_scales, q_norm_
             nc.gpsimd.tensor_tensor(out=sd[i][:, 0:1], in0=st[i][:, 1:2], in1=mhalf[:], op=ALU.pow)
 
         def apply(i, n, b):
-            nc.vector.scalar_tensor_tensor(
-                out=cn[i][:, 512 * n : 512 * (n + 1)],
-                in0=b[:],
-                scalar=sd[i][:, 0:1],
-                in1=wb[:, 512 * n : 512 * (n + 1)],
-                op0=ALU.mult,
-                op1=ALU.mult,
-            )
+            for u in range(2):
+                o = 512 * n + 256 * u
+                nc.vector.scalar_tensor_tensor(
+                    out=cn[i][:, o : o + 256].rearrange("p (m e) -> p m e", e=2),
+                    in0=b[:].rearrange("p (m u e) -> p u m e", u=2, e=2)[:, u, :, :],
+                    scalar=sd[i][:, 0:1],
+                    in1=wb[:, o : o + 256].rearrange("p (m e) -> p m e", e=2),
+                    op0=ALU.mult,
+                    op1=ALU.mult,
+                )
 
         def turn_c(i, g, b, slot):
             words = cn[i][:].bitcast(F32)
             for u in range(2):
                 o = (2 * slot + u) * P
-                nc.tensor.transpose(b[:, o : o + P], words[:, 256 * g + u : 256 * (g + 1) : 2], ident[:])
+                nc.tensor.transpose(b[:, o : o + P], words[:, 256 * g + P * u : 256 * g + P * (u + 1)], ident[:])
 
         def out_c(i, g0, g1, b):
             n = g1 - g0
@@ -232,7 +251,7 @@ def tile_mla_pa_w4_kernel(tc, x_bytes, x_scale, wq_a_words, wq_a_scales, q_norm_
                     lhsT=cq[i][:, g, :].bitcast(FP8X4),
                     lhsT_scale=cqs[i][:, g, :],
                     rhs=bw[k // 4][g][:, 1024 * kk : 1024 * (kk + 1)].bitcast(FP4X4),
-                    rhs_scale=bsc[:, g, 512 * k : 512 * (k + 1)],
+                    rhs_scale=bsc[k // 4][:, g, 512 * kk : 512 * (kk + 1)],
                     start=(g == 0),
                     stop=(g == GB - 1),
                 )
@@ -271,7 +290,7 @@ def tile_mla_pa_w4_kernel(tc, x_bytes, x_scale, wq_a_words, wq_a_scales, q_norm_
 
         def spread_w(n, b, half):
             nc.tensor.matmul(
-                b[:].bitcast(BF16)[:, 512 * half : 512 * (half + 1)], pick[:, n : n + 1].to_broadcast([P, P]), wrow[:], start=True, stop=True
+                b[:].bitcast(BF16)[:, 512 * half : 512 * (half + 1)], pick[:, n : n + 1].to_broadcast([P, P]), wrow[:].rearrange("p (m u e) -> p u m e", u=2, e=2), start=True, stop=True
             )
 
         def head_mm(g):
@@ -292,30 +311,21 @@ def tile_mla_pa_w4_kernel(tc, x_bytes, x_scale, wq_a_words, wq_a_scales, q_norm_
         quant(xq[0], xqs[0], xg[0], 3, 4)
         nc.vector.tensor_scalar(out=ang[:, 1, :, :], in0=raw[:], scalar1=0.01, scalar2=None, op0=ALU.mult)
         nc.vector.tensor_tensor(out=ang[:, 0, :, :], in0=raw[:], in1=rot[:], op=ALU.subtract)
-        zero_bsc(2)
-        zero_bsc(3)
-        zero_bsc(4)
-        zero_bsc(5)
-        for q in range(4):
-            nc.sync.dma_start(
-                out=bsc[32 * q : 32 * q + 4, :, :].bitcast(I32),
-                in_=wq_b_scales[:, 4 * q : 4 * q + 4, :].rearrange("g r n -> r g n").bitcast(I32),
-            )
-        for hf in range(2):
-            for g in range(GB):
-                nc.sync.dma_start(out=bw[hf][g][:].bitcast(I32), in_=wq_b_words[g][:, NQ * hf : NQ * (hf + 1)].bitcast(I32))
-            if hf == 0:
-                load_x(3)
+        for g in range(GB):
+            zero_bsc(1, g)
+        load_bsc(1)
+        load_x(3)
+        load_bw(1)
         tables()
         twin(1)
         t1 = [bank(4), bank(5)]
         head_mm(0)
+        head_mm(1)
         wa = bank(7)
         wc = bank(3)
         spread_w(0, wa, 0)
         spread_w(1, wa, 1)
         spread_w(2, wc, 0)
-        head_mm(1)
         for g in range(GA):
             turn_x(1, g, t1[g // 2], g % 2)
         for n in range(NA):

@@ -4,12 +4,13 @@ from contextlib import ExitStack
 import concourse.mybir as mybir
 from concourse.masks import make_identity
 
-T, DIM, QL, H, DH = 512, 2048, 1536, 16, 256
-NQ = H * DH
+TOKENS, DIM, QL, HEADS, HEAD = 512, 2048, 1536, 16, 256
+NQ = HEADS * HEAD
 HALF = 64
-P0 = 37
+LOW = 32
+POS0 = 37
 EPS = 1e-6
-FLOPS = 2 * T * DIM * QL + 2 * T * QL * NQ
+FLOPS = 2 * TOKENS * DIM * QL + 2 * TOKENS * QL * NQ
 
 F32 = mybir.dt.float32
 BF16 = mybir.dt.bfloat16
@@ -23,12 +24,48 @@ ALU = mybir.AluOpType
 ACT = mybir.ActivationFunctionType
 
 P = 128
-WARM = 5
-NT = T // P
-GA = DIM // 512
-GB = QL // 512
-NA = QL // 512
-NB = NQ // 512
+TILES = TOKENS // P
+PASSES_A = DIM // 512
+PASSES_B = QL // 512
+GROUPS_A = QL // 512
+GROUPS_B = NQ // 512
+WARM_UP = 5
+
+RING = (0, 7, 3, 1, 2)
+FIRST_BANKS = (6, 4, 5)
+
+SCHEDULE = {
+    (0, 0): (("cast_x", 3, 0), ("cast_x", 3, 1), ("scale_x", 2, 1), ("scale_x", 2, 2), ("scale_x", 2, 3), ("rstd", 1)),
+    (0, 2): (("quant_x", 2, 0), ("quant_x", 2, 1)),
+    (0, 3): (("norm", 1, 0), ("norm", 1, 1), ("norm", 1, 2)),
+    (0, 5): (("turn_x", 3), ("turn_c", 1), ("copy_c", 1, 0), ("copy_c", 1, 1), ("first", 2, 0)),
+    (0, 6): (
+        ("scale_x", 3, 0),
+        ("square", 2, 0),
+        ("quant_c", 1, 0),
+        ("quant_c", 1, 1),
+        ("first", 2, 1),
+        ("scale_x", 3, 1),
+        ("square", 2, 1),
+    ),
+    (0, 7): (("first", 2, 2),),
+    (1, 0): (("scale_x", 3, 2), ("scale_x", 3, 3), ("square", 2, 2), ("rstd", 2), ("quant_x", 3, 0)),
+    (1, 1): (("norm", 2, 0), ("norm", 2, 1), ("norm", 2, 2)),
+    (1, 4): (("turn_c", 2), ("copy_c", 2, 0), ("quant_x", 3, 1), ("copy_c", 2, 1)),
+    (1, 6): (
+        ("first", 3, 0),
+        ("first", 3, 1),
+        ("square", 3, 0),
+        ("square", 3, 1),
+        ("quant_c", 2, 0),
+        ("quant_c", 2, 1),
+        ("first", 3, 2),
+    ),
+    (1, 7): (("square", 3, 2), ("rstd", 3)),
+    (2, 0): (("norm", 3, 0), ("norm", 3, 1), ("norm", 3, 2)),
+    (2, 2): (("turn_c", 3), ("copy_c", 3, 0), ("copy_c", 3, 1)),
+    (2, 4): (("quant_c", 3, 0), ("quant_c", 3, 1)),
+}
 
 
 def tile_mla_pa_w4_kernel(tc, x_bytes, x_scale, wq_a_words, wq_a_scales, q_norm_w, wq_b_words, wq_b_scales, out):
@@ -45,398 +82,423 @@ def tile_mla_pa_w4_kernel(tc, x_bytes, x_scale, wq_a_words, wq_a_scales, q_norm_
         def bank(k):
             return psum.tile([P, 512], F32, name="bank%d" % k, tag="bank%d" % k)
 
-        def kt(shape, dt, name):
-            return keep.tile(shape, dt, name=name, align_bytes=256 if shape[-1] >= 128 else 64)
+        def kept(shape, dtype, name):
+            return keep.tile(shape, dtype, name=name, align_bytes=256 if shape[-1] >= P else 64)
 
-        xb = [kt([P, DIM], U8, "xb%d" % i) for i in range(NT)]
-        xw = [kt([P, DIM], BF16, "xw%d" % i) for i in range(NT)]
-        xg = [kt([P, GA, 512], BF16, "xg%d" % i) for i in range(NT)]
-        xq = [kt([P, GA, P], U32, "xq%d" % i) for i in range(NT)]
-        xqs = [kt([P, GA, P], U8, "xqs%d" % i) for i in range(NT)]
-        cn = [kt([P, QL], BF16, "cn%d" % i) for i in range(NT)]
-        cg = [kt([P, GB, 512], BF16, "cg%d" % i) for i in range(NT)]
-        cq = [kt([P, GB, P], U32, "cq%d" % i) for i in range(NT)]
-        cqs = [kt([P, GB, P], U8, "cqs%d" % i) for i in range(NT)]
-        ss = [kt([P, 4], F32, "ss%d" % i) for i in range(NT)]
-        st = [kt([P, 4], F32, "st%d" % i) for i in range(NT)]
-        sd = [kt([P, 4], F32, "sd%d" % i) for i in range(NT)]
-        xs = kt([P, GA, 4], F32, "xs")
-        aw = [kt([P, 2 * QL], U8, "aw%d" % g) for g in range(GA)]
-        asc = kt([P, GA, QL], U8, "asc")
-        bw = [[kt([P, NQ], U8, "bw%d_%d" % (hf, g)) for g in range(GB)] for hf in range(2)]
-        bsc = [kt([P, GB, NQ // 2], U8, "bsc%d" % h) for h in range(2)]
-        wb = kt([P, QL], BF16, "wb")
-        wrow = kt([P, 512], BF16, "wrow")
-        pick = kt([P, NA], BF16, "pick")
-        zero = kt([P, 512], BF16, "zero")
-        mhalf = kt([P, 1], F32, "mhalf")
-        ident = kt([P, P], F32, "ident")
-        posi = kt([P, H], I32, "posi")
-        posm = kt([P, H], I32, "posm")
-        posf = kt([P, H], F32, "posf")
-        th = kt([P, HALF // 2], F32, "th")
-        raw = kt([P, H, HALF // 2], F32, "raw")
-        ang = kt([P, 2, H, HALF // 2], F32, "ang")
-        rot = kt([P, H, HALF // 2], I32, "rot")
-        aab = kt([P, H, HALF // 2], F32, "aab")
-        tab = kt([P, 2, H, 2, HALF], F32, "tab")
-        dummy = kt([P, 1], F32, "dummy")
-        one = kt([P, 1], F32, "one")
+        x_raw = [kept([P, DIM], U8, "x_raw%d" % i) for i in range(TILES)]
+        x_wide = [kept([P, DIM], BF16, "x_wide%d" % i) for i in range(TILES)]
+        x_turned = [kept([P, PASSES_A, 512], BF16, "x_turned%d" % i) for i in range(TILES)]
+        x_codes = [kept([P, PASSES_A, P], U32, "x_codes%d" % i) for i in range(TILES)]
+        x_planes = [kept([P, PASSES_A, P], U8, "x_planes%d" % i) for i in range(TILES)]
+        cn = [kept([P, QL], BF16, "cn%d" % i) for i in range(TILES)]
+        c_turned = [kept([P, PASSES_B, 512], BF16, "c_turned%d" % i) for i in range(TILES)]
+        c_codes = [kept([P, PASSES_B, P], U32, "c_codes%d" % i) for i in range(TILES)]
+        c_planes = [kept([P, PASSES_B, P], U8, "c_planes%d" % i) for i in range(TILES)]
+        parts = [kept([P, GROUPS_A], F32, "parts%d" % i) for i in range(TILES)]
+        sums = [kept([P, 2], F32, "sums%d" % i) for i in range(TILES)]
+        inv_rms = [kept([P, 1], F32, "inv_rms%d" % i) for i in range(TILES)]
 
-        nc.gpsimd.memset(zero[:].bitcast(I32), 0)
-        nc.gpsimd.iota(posi[:], pattern=[[1, H]], base=0, channel_multiplier=16)
-        for k in range(WARM):
-            nc.tensor.matmul(bank(7)[:], zero[:, 0:P], zero[:], start=True, stop=True)
-        nc.vector.memset(one[:], 1.0)
+        a_words = [kept([P, 2 * QL], U8, "a_words%d" % g) for g in range(PASSES_A)]
+        a_planes = kept([P, PASSES_A, QL], U8, "a_planes")
+        b_words = [[kept([P, NQ], U8, "b_words%d_%d" % (h, g)) for g in range(PASSES_B)] for h in range(2)]
+        b_planes = [kept([P, PASSES_B, NQ // 2], U8, "b_planes%d" % h) for h in range(2)]
+        scales = kept([P, PASSES_A, 4], F32, "scales")
+        gain = kept([P, QL], BF16, "gain")
 
-        def zero_asc(g0, g1):
-            nc.vector.memset(asc[:, g0:g1, :].rearrange("p g n -> p (g n)").bitcast(I32), 0)
+        gain_rows = kept([P, 512], BF16, "gain_rows")
+        pick = kept([P, GROUPS_A], BF16, "pick")
+        ident = kept([P, P], F32, "ident")
+        zeros = kept([P, 512], BF16, "zeros")
+        one = kept([P, 1], F32, "one")
+        minus_half = kept([P, 1], F32, "minus_half")
+        table_load = kept([P, 1], F32, "table_load")
 
-        def zero_bsc(h, g):
-            nc.vector.memset(bsc[h][:, g, :].bitcast(I32), 0)
+        row = kept([P, HEADS], I32, "row")
+        row_mod = kept([P, HEADS], I32, "row_mod")
+        position = kept([P, HEADS], F32, "position")
+        freq = kept([P, LOW], F32, "freq")
+        turns = kept([P, HEADS, LOW], F32, "turns")
+        whole = kept([P, HEADS, LOW], I32, "whole")
+        angle = kept([P, 2, HEADS, LOW], F32, "angle")
+        angle_abs = kept([P, HEADS, LOW], F32, "angle_abs")
+        table = kept([P, 2, HEADS, 2, HALF], F32, "table")
 
-        def load_asc(g0, g1):
+        def load_x(i):
+            nc.sync.dma_start(out=x_raw[i][:], in_=x_rows[P * i : P * (i + 1), :])
+
+        def load_a_words(g):
+            nc.sync.dma_start(out=a_words[g][:].bitcast(I32), in_=wq_a_words[g].bitcast(I32))
+
+        def load_b_words(h):
+            for g in range(PASSES_B):
+                nc.sync.dma_start(out=b_words[h][g][:].bitcast(I32), in_=wq_b_words[g][:, NQ * h : NQ * (h + 1)].bitcast(I32))
+
+        def zero_a_planes(g0, g1):
+            nc.vector.memset(a_planes[:, g0:g1, :].rearrange("p g n -> p (g n)").bitcast(I32), 0)
+
+        def load_a_planes(g0, g1):
             for q in range(4):
                 nc.sync.dma_start(
-                    out=asc[32 * q : 32 * q + 4, g0:g1, :].bitcast(I32),
+                    out=a_planes[32 * q : 32 * q + 4, g0:g1, :].bitcast(I32),
                     in_=wq_a_scales[g0:g1, 4 * q : 4 * q + 4, :].rearrange("g r n -> r g n").bitcast(I32),
                 )
 
-        def load_bsc(h):
+        def zero_b_planes(h, g):
+            nc.vector.memset(b_planes[h][:, g, :].bitcast(I32), 0)
+
+        def load_b_planes(h):
+            n0 = h * NQ // 2
             for q in range(4):
                 nc.sync.dma_start(
-                    out=bsc[h][32 * q : 32 * q + 4, :, :].bitcast(I32),
-                    in_=wq_b_scales[:, 4 * q : 4 * q + 4, 2048 * h : 2048 * (h + 1)].rearrange("g r n -> r g n").bitcast(I32),
+                    out=b_planes[h][32 * q : 32 * q + 4, :, :].bitcast(I32),
+                    in_=wq_b_scales[:, 4 * q : 4 * q + 4, n0 : n0 + NQ // 2].rearrange("g r n -> r g n").bitcast(I32),
                 )
 
-        def load_aw(g):
-            nc.sync.dma_start(out=aw[g][:].bitcast(I32), in_=wq_a_words[g].bitcast(I32))
-
-        def load_bw(h):
-            for g in range(GB):
-                nc.sync.dma_start(out=bw[h][g][:].bitcast(I32), in_=wq_b_words[g][:, NQ * h : NQ * (h + 1)].bitcast(I32))
-
-        def load_x(i):
-            nc.sync.dma_start(out=xb[i][:], in_=x_rows[P * i : P * (i + 1), :])
-
-        nc.gpsimd.memset(wrow[:].bitcast(I32), 0)
-        zero_asc(0, 2)
-        load_x(0)
-        load_asc(0, 2)
-        load_aw(0)
-        nc.sync.dma_start(out=xs[:], in_=x_scale.rearrange("a b (g p t) -> (a b p) g t", p=P, t=4))
-        nc.sync.dma_start(out=wrow[0:NA, :], in_=q_norm_w.rearrange("(r c) -> r c", r=NA))
-        load_aw(1)
-        load_x(1)
-        nc.vector.tensor_scalar(out=posm[:], in0=posi[:], scalar1=255, scalar2=None, op0=ALU.bitwise_and)
-        nc.vector.tensor_scalar(out=th[:, 0:1], in0=one[:], scalar1=0.5 / math.pi, scalar2=None, op0=ALU.mult)
-        zero_asc(2, 4)
-        load_asc(2, 4)
-        load_aw(2)
-        load_aw(3)
-        for m in (1, 2, 3):
-            nc.vector.tensor_scalar(out=th[:, m : m + 1], in0=th[:, 0:1], scalar1=10000.0 ** (-m / 64.0), scalar2=None, op0=ALU.mult)
-        nc.vector.tensor_scalar(out=posf[:], in0=posm[:], scalar1=float(P0), scalar2=None, op0=ALU.add)
-        zero_bsc(0, 0)
-        for m in (1, 2, 3):
+        def scale_freq(j0, j1, width):
             nc.vector.tensor_scalar(
-                out=th[:, 4 * m : 4 * m + 4], in0=th[:, 0:4], scalar1=10000.0 ** (-4 * m / 64.0), scalar2=None, op0=ALU.mult
+                out=freq[:, j0:j1], in0=freq[:, 0:width], scalar1=10000.0 ** (-j0 / 64.0), scalar2=None, op0=ALU.mult
             )
-        zero_bsc(0, 1)
-        nc.vector.tensor_scalar(out=th[:, 16:32], in0=th[:, 0:16], scalar1=10000.0 ** (-16 / 64.0), scalar2=None, op0=ALU.mult)
-        zero_bsc(0, 2)
-        load_bsc(0)
-        load_x(2)
-        load_bw(0)
-        nc.scalar.activation(out=dummy[:], in_=one[:], func=ACT.Sin)
-        nc.vector.tensor_tensor(
-            out=raw[:],
-            in0=posf[:].unsqueeze(2).to_broadcast([P, H, HALF // 2]),
-            in1=th[:].unsqueeze(1).to_broadcast([P, H, HALF // 2]),
-            op=ALU.mult,
-        )
-        make_identity(nc, ident[:])
-        nc.gpsimd.memset(mhalf[:], -0.5)
-        nc.gpsimd.tensor_copy(out=pick[:], in_=ident[:, 0:NA])
 
-        def tables():
-            nc.scalar.activation(
-                out=tab[:, 1, :, 0, :].rearrange("p h (a j) -> p a h j", a=2), in_=ang[:], func=ACT.Sin, scale=2.0 * math.pi
-            )
-            nc.scalar.activation(out=aab[:], in_=ang[:, 0, :, :], func=ACT.Abs)
-            for a, src in ((0, aab[:]), (1, ang[:, 1, :, :])):
+        def spread(ap):
+            return ap.rearrange("p h (a j) -> p a h j", a=2)
+
+        def sine_tables():
+            nc.scalar.activation(out=spread(table[:, 1, :, 0, :]), in_=angle[:], func=ACT.Sin, scale=2.0 * math.pi)
+            nc.scalar.activation(out=angle_abs[:], in_=angle[:, 0, :, :], func=ACT.Abs)
+            for a, size in ((0, angle_abs[:]), (1, angle[:, 1, :, :])):
                 nc.scalar.activation(
-                    out=tab[:, 0, :, 0, 32 * a : 32 * a + 32], in_=src, func=ACT.Sin, scale=-2.0 * math.pi, bias=0.5 * math.pi
+                    out=table[:, 0, :, 0, LOW * a : LOW * (a + 1)],
+                    in_=size,
+                    func=ACT.Sin,
+                    scale=-2.0 * math.pi,
+                    bias=0.5 * math.pi,
                 )
 
-        def twin(w):
-            nc.gpsimd.tensor_scalar(out=tab[:, w, :, 1, :], in0=tab[:, w, :, 0, :], scalar1=1.0, scalar2=0.0, op0=ALU.mult, op1=ALU.add)
+        def repeat_table(w):
+            nc.gpsimd.tensor_scalar(
+                out=table[:, w, :, 1, :], in0=table[:, w, :, 0, :], scalar1=1.0, scalar2=0.0, op0=ALU.mult, op1=ALU.add
+            )
 
-        def cast_x(i, c0, c1):
-            nc.scalar.copy(out=xw[i][:, c0:c1], in_=xb[i][:, c0:c1].bitcast(F8))
+        x_banks = {}
 
-        def turn_x(i, g, b, slot):
-            words = xw[i][:].bitcast(F32)
+        def widen_x(i, k0, k1):
+            nc.scalar.copy(out=x_wide[i][:, k0:k1], in_=x_raw[i][:, k0:k1].bitcast(F8))
+
+        def cast_x(i, part):
+            widen_x(i, 1024 * part, 1024 * (part + 1))
+
+        def turn_pass(i, g, b, slot):
+            words = x_wide[i][:].bitcast(F32)
             for u in range(2):
                 o = (2 * slot + u) * P
                 nc.tensor.transpose(b[:, o : o + P], words[:, 256 * g + u : 256 * (g + 1) : 2], ident[:])
 
-        def scale_x(i, g, b, slot):
+        def turn_x(i):
+            x_banks[i] = [next_bank(), next_bank()]
+            for g in range(PASSES_A):
+                turn_pass(i, g, x_banks[i][g // 2], g % 2)
+
+        def scale_pass(i, g, b, slot):
             nc.vector.tensor_tensor(
-                out=xg[i][:, g, :].rearrange("p (r u e) -> p r u e", u=2, e=2),
+                out=x_turned[i][:, g, :].rearrange("p (r u e) -> p r u e", u=2, e=2),
                 in0=b[:, 256 * slot : 256 * (slot + 1)].bitcast(BF16).rearrange("p (u r e) -> p r u e", u=2, e=2),
-                in1=xs[:, g, :].rearrange("p (u e) -> p u e", e=2).unsqueeze(1).to_broadcast([P, P, 2, 2]),
+                in1=scales[:, g, :].rearrange("p (u e) -> p u e", e=2).unsqueeze(1).to_broadcast([P, P, 2, 2]),
                 op=ALU.mult,
             )
 
-        def quant(dst, sc, src, g0, g1):
+        def scale_x(i, g):
+            scale_pass(i, g, x_banks[i][g // 2], g % 2)
+
+        def quantize(codes, planes, values, g0, g1):
             nc.vector.quantize_mx(
-                out=dst[:, g0:g1, :].rearrange("p g c -> p (g c)").bitcast(FP8X4),
-                scales=sc[:, g0:g1, :].rearrange("p g c -> p (g c)"),
-                in_=src[:, g0:g1, :].rearrange("p g c -> p (g c)"),
+                out=codes[:, g0:g1, :].rearrange("p g r -> p (g r)").bitcast(FP8X4),
+                scales=planes[:, g0:g1, :].rearrange("p g r -> p (g r)"),
+                in_=values[:, g0:g1, :].rearrange("p g c -> p (g c)"),
             )
 
-        def mm1(i, g, n, b):
+        def quantize_x(i, g0, g1):
+            quantize(x_codes[i], x_planes[i], x_turned[i], g0, g1)
+
+        def quant_x(i, part):
+            quantize_x(i, 2 * part, 2 * part + 2)
+
+        c_banks = {}
+
+        def first_pass(i, g, n, b):
             nc.tensor.matmul_mx(
                 out=b[:],
-                lhsT=xq[i][:, g, :].bitcast(FP8X4),
-                lhsT_scale=xqs[i][:, g, :],
-                rhs=aw[g][:, 1024 * n : 1024 * (n + 1)].bitcast(FP4X4),
-                rhs_scale=asc[:, g, 512 * n : 512 * (n + 1)],
+                lhsT=x_codes[i][:, g, :].bitcast(FP8X4),
+                lhsT_scale=x_planes[i][:, g, :],
+                rhs=a_words[g][:, 1024 * n : 1024 * (n + 1)].bitcast(FP4X4),
+                rhs_scale=a_planes[:, g, 512 * n : 512 * (n + 1)],
                 start=(g == 0),
-                stop=(g == GA - 1),
+                stop=(g == PASSES_A - 1),
             )
 
-        def square(i, n, b):
+        def first(i, n):
+            b = bank(FIRST_BANKS[n])
+            c_banks.setdefault(i, []).append(b)
+            for g in range(PASSES_A):
+                first_pass(i, g, n, b)
+
+        def square(i, n):
             junk = work.tile([P, 512], BF16, name="junk")
-            nc.scalar.activation(out=junk[:], in_=b[:], func=ACT.Square, scale=QL ** -0.5, accum_out=ss[i][:, n : n + 1])
-
-        def total(i):
-            nc.vector.scalar_tensor_tensor(
-                out=st[i][:, 0:1], in0=ss[i][:, 0:1], scalar=EPS, in1=ss[i][:, 1:2], op0=ALU.add, op1=ALU.add
+            nc.scalar.activation(
+                out=junk[:], in_=c_banks[i][n][:], func=ACT.Square, scale=QL**-0.5, accum_out=parts[i][:, n : n + 1]
             )
-            nc.vector.tensor_tensor(out=st[i][:, 1:2], in0=st[i][:, 0:1], in1=ss[i][:, 2:3], op=ALU.add)
-            nc.gpsimd.tensor_tensor(out=sd[i][:, 0:1], in0=st[i][:, 1:2], in1=mhalf[:], op=ALU.pow)
 
-        def apply(i, n, b):
+        def add_parts(i):
+            nc.vector.scalar_tensor_tensor(
+                out=sums[i][:, 0:1], in0=parts[i][:, 0:1], scalar=EPS, in1=parts[i][:, 1:2], op0=ALU.add, op1=ALU.add
+            )
+
+        def invert(i):
+            nc.vector.tensor_tensor(out=sums[i][:, 1:2], in0=sums[i][:, 0:1], in1=parts[i][:, 2:3], op=ALU.add)
+            nc.gpsimd.tensor_tensor(out=inv_rms[i][:], in0=sums[i][:, 1:2], in1=minus_half[:], op=ALU.pow)
+
+        def rstd(i):
+            add_parts(i)
+            invert(i)
+
+        def norm(i, n):
             for u in range(2):
-                o = 512 * n + 256 * u
+                cols = slice(512 * n + 256 * u, 512 * n + 256 * (u + 1))
                 nc.vector.scalar_tensor_tensor(
-                    out=cn[i][:, o : o + 256].rearrange("p (m e) -> p m e", e=2),
-                    in0=b[:].rearrange("p (m u e) -> p u m e", u=2, e=2)[:, u, :, :],
-                    scalar=sd[i][:, 0:1],
-                    in1=wb[:, o : o + 256].rearrange("p (m e) -> p m e", e=2),
+                    out=cn[i][:, cols].rearrange("p (m e) -> p m e", e=2),
+                    in0=c_banks[i][n][:].rearrange("p (m u e) -> p u m e", u=2, e=2)[:, u, :, :],
+                    scalar=inv_rms[i][:],
+                    in1=gain[:, cols].rearrange("p (m e) -> p m e", e=2),
                     op0=ALU.mult,
                     op1=ALU.mult,
                 )
 
-        def turn_c(i, g, b, slot):
+        cn_banks = {}
+
+        def turn_cn_pass(i, g, b, slot):
             words = cn[i][:].bitcast(F32)
             for u in range(2):
                 o = (2 * slot + u) * P
                 nc.tensor.transpose(b[:, o : o + P], words[:, 256 * g + P * u : 256 * g + P * (u + 1)], ident[:])
 
-        def out_c(i, g0, g1, b):
-            n = g1 - g0
+        def copy_cn(i, g0, g1, b):
             nc.scalar.copy(
-                out=cg[i][:, g0:g1, :].bitcast(F32).rearrange("p g (r u) -> p g r u", u=2),
-                in_=b[:, 0 : 256 * n].rearrange("p (g u r) -> p g r u", u=2, r=P),
+                out=c_turned[i][:, g0:g1, :].bitcast(F32).rearrange("p g (r u) -> p g r u", u=2),
+                in_=b[:, 0 : 256 * (g1 - g0)].rearrange("p (g u r) -> p g r u", u=2, r=P),
             )
 
-        def mm2(i, k, b):
-            for g in range(GB):
-                kk = k % 4
+        def quantize_c(i, g0, g1):
+            quantize(c_codes[i], c_planes[i], c_turned[i], g0, g1)
+
+        def turn_c(i):
+            cn_banks[i] = [bank(FIRST_BANKS[1]), bank(FIRST_BANKS[2])]
+            for g in range(PASSES_B):
+                turn_cn_pass(i, g, cn_banks[i][g // 2], g % 2)
+
+        def copy_c(i, part):
+            copy_cn(i, 2 * part, min(2 * part + 2, PASSES_B), cn_banks[i][part])
+
+        def quant_c(i, part):
+            quantize_c(i, 2 * part, min(2 * part + 2, PASSES_B))
+
+        def second(i, k, b):
+            h, kk = divmod(k, GROUPS_B // 2)
+            for g in range(PASSES_B):
                 nc.tensor.matmul_mx(
                     out=b[:],
-                    lhsT=cq[i][:, g, :].bitcast(FP8X4),
-                    lhsT_scale=cqs[i][:, g, :],
-                    rhs=bw[k // 4][g][:, 1024 * kk : 1024 * (kk + 1)].bitcast(FP4X4),
-                    rhs_scale=bsc[k // 4][:, g, 512 * kk : 512 * (kk + 1)],
+                    lhsT=c_codes[i][:, g, :].bitcast(FP8X4),
+                    lhsT_scale=c_planes[i][:, g, :],
+                    rhs=b_words[h][g][:, 1024 * kk : 1024 * (kk + 1)].bitcast(FP4X4),
+                    rhs_scale=b_planes[h][:, g, 512 * kk : 512 * (kk + 1)],
                     start=(g == 0),
-                    stop=(g == GB - 1),
+                    stop=(g == PASSES_B - 1),
                 )
 
-        state = {}
+        pair = {}
 
-        def rope(i, k, b):
+        def finish(i, k, b):
             s = k % 2
             if s == 0:
-                state["res"] = work.tile([P, 4, 2, 2, HALF], F32, name="res", bufs=8)
-                state["t"] = work.tile([P, 4, 2, 2, HALF], F32, name="t", bufs=4)
-            res, t = state["res"], state["t"]
-            v = b[:].rearrange("p (h x c) -> p h x c", h=2, x=2)
-            hs = slice(2 * s, 2 * s + 2)
+                pair["result"] = work.tile([P, 4, 2, 2, HALF], F32, name="result", bufs=8)
+                pair["terms"] = work.tile([P, 4, 2, 2, HALF], F32, name="terms", bufs=4)
+            result, terms = pair["result"], pair["terms"]
+            alone = i == TILES - 1 and k >= GROUPS_B - 2
+            heads = slice(2 * s, 2 * s + 2)
+            halves = b[:].rearrange("p (h x c) -> p h x c", h=2, x=2)
+
             nc.vector.tensor_tensor(
-                out=t[:, hs, :, :, :].rearrange("p h w f j -> p w h (f j)"),
-                in0=v[:, :, 1, :].unsqueeze(1).to_broadcast([P, 2, 2, 2 * HALF]),
-                in1=tab[:, :, 2 * k : 2 * k + 2, :, :].rearrange("p w h f j -> p w h (f j)"),
+                out=terms[:, heads, :, :, :].rearrange("p h w f j -> p w h (f j)"),
+                in0=halves[:, :, 1, :].unsqueeze(1).to_broadcast([P, 2, 2, 2 * HALF]),
+                in1=table[:, :, 2 * k : 2 * k + 2, :, :].rearrange("p w h f j -> p w h (f j)"),
                 op=ALU.mult,
             )
-            nc.scalar.copy(out=res[:, hs, 0, :, :].rearrange("p h f j -> p h (f j)"), in_=v[:, :, 0, :])
-            last = i == NT - 1 and k >= NB - 2
-            if s == 1 or last:
-                hs = slice(2 * s, 2 * s + 2) if last else slice(0, 4)
-                eng = nc.vector if last and s == 1 else nc.gpsimd
-                eng.tensor_tensor(out=res[:, hs, 1, 0, :], in0=t[:, hs, 0, 0, :], in1=t[:, hs, 1, 1, :], op=ALU.subtract)
-                eng.tensor_tensor(out=res[:, hs, 1, 1, :], in0=t[:, hs, 0, 1, :], in1=t[:, hs, 1, 0, :], op=ALU.add)
-                n0 = 512 * k if last else 512 * (k - 1)
+            nc.scalar.copy(out=result[:, heads, 0, :, :].rearrange("p h f j -> p h (f j)"), in_=halves[:, :, 0, :])
+            if s == 1 or alone:
+                done = heads if alone else slice(0, 4)
+                engine = nc.vector if alone and s == 1 else nc.gpsimd
+                for f, op in ((0, ALU.subtract), (1, ALU.add)):
+                    engine.tensor_tensor(
+                        out=result[:, done, 1, f, :], in0=terms[:, done, 0, f, :], in1=terms[:, done, 1, 1 - f, :], op=op
+                    )
+                n0 = 512 * (k if alone else k - 1)
                 nc.sync.dma_start(
                     out=out_rows[P * i : P * (i + 1), n0 : 512 * (k + 1)],
-                    in_=res[:, hs, :, :, :].rearrange("p h x f j -> p (h x f j)"),
+                    in_=result[:, done, :, :, :].rearrange("p h x f j -> p (h x f j)"),
                 )
 
-        c0 = [bank(n) for n in range(NA)]
-        tb = [bank(3 + g) for g in range(GA)]
+        nc.gpsimd.memset(zeros[:].bitcast(I32), 0)
+        nc.gpsimd.iota(row[:], pattern=[[1, HEADS]], base=0, channel_multiplier=16)
+        for m in range(WARM_UP):
+            nc.tensor.matmul(bank(7)[:], zeros[:, 0:P], zeros[:], start=True, stop=True)
+        nc.vector.memset(one[:], 1.0)
+        nc.gpsimd.memset(gain_rows[:].bitcast(I32), 0)
 
-        def spread_w(n, b, half):
+        load_x(0)
+        nc.sync.dma_start(out=scales[:], in_=x_scale.rearrange("a b (g p t) -> (a b p) g t", p=P, t=4))
+        zero_a_planes(0, 2)
+        load_a_planes(0, 2)
+        load_a_words(0)
+        load_x(1)
+        nc.sync.dma_start(out=gain_rows[0:GROUPS_A, :], in_=q_norm_w.rearrange("(r c) -> r c", r=GROUPS_A))
+        load_a_words(1)
+        nc.vector.tensor_scalar(out=row_mod[:], in0=row[:], scalar1=255, scalar2=None, op0=ALU.bitwise_and)
+        nc.vector.tensor_scalar(out=freq[:, 0:1], in0=one[:], scalar1=0.5 / math.pi, scalar2=None, op0=ALU.mult)
+        zero_a_planes(2, 4)
+        load_a_planes(2, 4)
+        load_a_words(2)
+        load_a_words(3)
+        for m in (1, 2, 3):
+            scale_freq(m, m + 1, 1)
+        nc.vector.tensor_scalar(out=position[:], in0=row_mod[:], scalar1=float(POS0), scalar2=None, op0=ALU.add)
+        zero_b_planes(0, 0)
+        for m in (4, 8, 12):
+            scale_freq(m, m + 4, 4)
+        zero_b_planes(0, 1)
+        scale_freq(16, 32, 16)
+        nc.scalar.activation(out=table_load[:], in_=one[:], func=ACT.Sin)
+        nc.vector.tensor_tensor(
+            out=turns[:],
+            in0=position[:].unsqueeze(2).to_broadcast([P, HEADS, LOW]),
+            in1=freq[:].unsqueeze(1).to_broadcast([P, HEADS, LOW]),
+            op=ALU.mult,
+        )
+        make_identity(nc, ident[:])
+        nc.gpsimd.memset(minus_half[:], -0.5)
+        nc.gpsimd.tensor_copy(out=pick[:], in_=ident[:, 0:GROUPS_A])
+
+        c_banks[0] = [bank(n) for n in range(GROUPS_A)]
+        x0_banks = [bank(3 + g) for g in range(PASSES_A)]
+        for g in range(PASSES_A):
+            widen_x(0, 512 * g, 512 * (g + 1))
+        cast_x(1, 0)
+        cast_x(1, 1)
+        for g in range(PASSES_A):
+            turn_pass(0, g, x0_banks[g], 0)
+
+        scale_pass(0, 0, x0_banks[0], 0)
+        zero_b_planes(0, 2)
+        quantize_x(0, 0, 1)
+        scale_pass(0, 1, x0_banks[1], 0)
+        nc.vector.tensor_copy(out=whole[:], in_=turns[:])
+        quantize_x(0, 1, 2)
+        nc.vector.tensor_scalar(out=angle[:, 1, :, :], in0=turns[:], scalar1=0.01, scalar2=None, op0=ALU.mult)
+        nc.vector.tensor_tensor(out=angle[:, 0, :, :], in0=turns[:], in1=whole[:], op=ALU.subtract)
+        scale_pass(0, 2, x0_banks[2], 0)
+        scale_pass(0, 3, x0_banks[3], 0)
+        quantize_x(0, 2, 3)
+        load_b_planes(0)
+        load_x(2)
+        load_b_words(0)
+        load_x(3)
+        load_b_words(1)
+        zero_b_planes(1, 0)
+        quantize_x(0, 3, 4)
+        sine_tables()
+        repeat_table(1)
+
+        x_banks[1] = [bank(4), bank(5)]
+        for g in range(2):
+            for n in range(GROUPS_A):
+                first_pass(0, g, n, c_banks[0][n])
+        for g in range(PASSES_A):
+            turn_pass(1, g, x_banks[1][g // 2], g % 2)
+        for n in range(GROUPS_A):
+            first_pass(0, 2, n, c_banks[0][n])
+            first_pass(0, 3, n, c_banks[0][n])
+            square(0, n)
+
+        gain_bank, gain_bank_2 = bank(7), bank(3)
+        for n, b, o in ((0, gain_bank, 0), (1, gain_bank, 512), (2, gain_bank_2, 0)):
             nc.tensor.matmul(
-                b[:].bitcast(BF16)[:, 512 * half : 512 * (half + 1)], pick[:, n : n + 1].to_broadcast([P, P]), wrow[:].rearrange("p (m u e) -> p u m e", u=2, e=2), start=True, stop=True
+                b[:].bitcast(BF16)[:, o : o + 512],
+                pick[:, n : n + 1].to_broadcast([P, P]),
+                gain_rows[:].rearrange("p (m u e) -> p u m e", u=2, e=2),
+                start=True,
+                stop=True,
             )
 
-        def head_mm(g):
-            for n in range(NA):
-                mm1(0, g, n, c0[n])
+        for g in range(3):
+            scale_x(1, g)
+        quant_x(1, 0)
+        scale_x(1, 3)
+        zero_b_planes(1, 1)
+        quant_x(1, 1)
+        nc.vector.tensor_copy(out=gain[:, 0:1024], in_=gain_bank[:].bitcast(BF16))
+        nc.scalar.copy(out=gain[:, 1024:QL], in_=gain_bank_2[:, 0:256].bitcast(BF16))
+        add_parts(0)
+        zero_b_planes(1, 2)
+        invert(0)
+        load_b_planes(1)
+        repeat_table(0)
+        cast_x(2, 0)
+        cast_x(2, 1)
+        for n in range(GROUPS_A):
+            norm(0, n)
 
-        for g in range(GA):
-            cast_x(0, 512 * g, 512 * (g + 1))
-        cast_x(1, 0, 1024)
-        cast_x(1, 1024, 2048)
-        for g in range(GA):
-            turn_x(0, g, tb[g], 0)
-        for g in range(GA):
-            scale_x(0, g, tb[g], 0)
-            if g > 0:
-                quant(xq[0], xqs[0], xg[0], g - 1, g)
-        nc.vector.tensor_copy(out=rot[:], in_=raw[:])
-        quant(xq[0], xqs[0], xg[0], 3, 4)
-        nc.vector.tensor_scalar(out=ang[:, 1, :, :], in0=raw[:], scalar1=0.01, scalar2=None, op0=ALU.mult)
-        nc.vector.tensor_tensor(out=ang[:, 0, :, :], in0=raw[:], in1=rot[:], op=ALU.subtract)
-        for g in range(GB):
-            zero_bsc(1, g)
-        load_bsc(1)
-        load_x(3)
-        load_bw(1)
-        tables()
-        twin(1)
-        t1 = [bank(4), bank(5)]
-        head_mm(0)
-        head_mm(1)
-        wa = bank(7)
-        wc = bank(3)
-        spread_w(0, wa, 0)
-        spread_w(1, wa, 1)
-        spread_w(2, wc, 0)
-        for g in range(GA):
-            turn_x(1, g, t1[g // 2], g % 2)
-        for n in range(NA):
-            mm1(0, 2, n, c0[n])
-            mm1(0, 3, n, c0[n])
-            square(0, n, c0[n])
-        for g in range(GA):
-            scale_x(1, g, t1[g // 2], g % 2)
-            if g == 2:
-                quant(xq[1], xqs[1], xg[1], 0, 2)
-        quant(xq[1], xqs[1], xg[1], 2, 4)
-        nc.vector.tensor_copy(out=wb[:, 0:1024], in_=wa[:].bitcast(BF16))
-        nc.scalar.copy(out=wb[:, 1024:1536], in_=wc[:, 0:256].bitcast(BF16))
-        total(0)
-        twin(0)
-        cast_x(2, 0, 1024)
-        for n in range(NA):
-            apply(0, n, c0[n])
-        c1 = [bank((6, 4, 5)[n]) for n in range(NA)]
-        for n in range(NA):
-            mm1(1, 0, n, c1[n])
-            mm1(1, 1, n, c1[n])
-        for n in range(NA):
-            mm1(1, 2, n, c1[n])
-            mm1(1, 3, n, c1[n])
-        tcs = [bank(0), bank(7), bank(3)]
-        for g in range(GB):
-            turn_c(0, g, tcs[g], 0)
-            out_c(0, g, g + 1, tcs[g])
-            quant(cq[0], cqs[0], cg[0], g, g + 1)
-        for n in range(NA):
-            square(1, n, c1[n])
+        c_banks[1] = [bank(FIRST_BANKS[n]) for n in range(GROUPS_A)]
+        for half in range(2):
+            for n in range(GROUPS_A):
+                first_pass(1, 2 * half, n, c_banks[1][n])
+                first_pass(1, 2 * half + 1, n, c_banks[1][n])
+        cn0_banks = [bank(k) for k in (0, 7, 3)]
+        for g in range(PASSES_B):
+            turn_cn_pass(0, g, cn0_banks[g], 0)
+        x_banks[2] = [bank(1), bank(2)]
+        for g in range(PASSES_A):
+            turn_pass(2, g, x_banks[2][g // 2], g % 2)
+        for g in range(PASSES_B):
+            copy_cn(0, g, g + 1, cn0_banks[g])
+            quantize_c(0, g, g + 1)
+        scale_x(2, 0)
+        for n in range(GROUPS_A):
+            square(1, n)
 
-        cur = {1: c1}
-        ring = [1, 2, 0, 7, 3]
-        cbank = [6, 4, 5]
-        cnt = [0]
-        tx = {}
-        tcb = {}
-        pend = []
+        turn = [0]
 
-        def nextbank():
-            b = bank(ring[cnt[0] % len(ring)])
-            cnt[0] += 1
-            return b
+        def next_bank():
+            turn[0] += 1
+            return bank(RING[(turn[0] - 1) % len(RING)])
 
-        def do(name, i, a=0):
-            if name == "total":
-                total(i)
-            elif name == "apply":
-                apply(i, a, cur[i][a])
-            elif name == "cast":
-                cast_x(i, 1024 * a, 1024 * (a + 1))
-            elif name == "turnx":
-                tx[i] = [nextbank(), nextbank()]
-                for g in range(GA):
-                    turn_x(i, g, tx[i][g // 2], g % 2)
-            elif name == "scalex":
-                scale_x(i, a, tx[i][a // 2], a % 2)
-            elif name == "quantx":
-                quant(xq[i], xqs[i], xg[i], 2 * a, 2 * a + 2)
-            elif name == "turnc":
-                tcb[i] = [bank(cbank[1]), bank(cbank[2])]
-                for g in range(GB):
-                    turn_c(i, g, tcb[i][g // 2], g % 2)
-            elif name == "outc":
-                if a == 0:
-                    out_c(i, 0, 2, tcb[i][0])
-                else:
-                    out_c(i, 2, 3, tcb[i][1])
-            elif name == "quantc":
-                if a == 0:
-                    quant(cq[i], cqs[i], cg[i], 0, 2)
-                else:
-                    quant(cq[i], cqs[i], cg[i], 2, 3)
-            elif name == "mm1":
-                b = bank(cbank[a])
-                cur.setdefault(i, []).append(b)
-                for g in range(GA):
-                    mm1(i, g, a, b)
-            elif name == "sq":
-                square(i, a, cur[i][a])
-
-        plan = {
-            (0, 0): [('cast', 2, 1)],
-            (0, 1): [('total', 1)],
-            (0, 3): [('apply', 1, 1)],
-            (0, 4): [('cast', 3, 0)],
-            (0, 5): [('apply', 1, 0), ('turnx', 2)],
-            (0, 6): [('apply', 1, 2), ('scalex', 2, 3), ('scalex', 2, 0), ('scalex', 2, 2), ('scalex', 2, 1), ('cast', 3, 1), ('turnc', 1), ('outc', 1, 1), ('outc', 1, 0), ('quantx', 2, 1), ('quantx', 2, 0), ('turnx', 3)],
-            (0, 7): [('mm1', 2, 0), ('mm1', 2, 1), ('quantc', 1, 0), ('quantc', 1, 1), ('mm1', 2, 2), ('scalex', 3, 3), ('scalex', 3, 2), ('scalex', 3, 1), ('sq', 2, 1), ('sq', 2, 0)],
-            (1, 0): [('quantx', 3, 1), ('sq', 2, 2), ('scalex', 3, 0)],
-            (1, 1): [('total', 2)],
-            (1, 2): [('apply', 2, 0)],
-            (1, 3): [('quantx', 3, 0), ('apply', 2, 1), ('apply', 2, 2)],
-            (1, 5): [('turnc', 2), ('outc', 2, 0), ('outc', 2, 1), ('mm1', 3, 0)],
-            (1, 6): [('quantc', 2, 1), ('quantc', 2, 0), ('sq', 3, 0), ('mm1', 3, 1), ('mm1', 3, 2), ('sq', 3, 1)],
-            (1, 7): [('sq', 3, 2), ('total', 3)],
-            (2, 0): [('apply', 3, 0)],
-            (2, 3): [('apply', 3, 1), ('apply', 3, 2)],
-            (2, 4): [('turnc', 3), ('outc', 3, 1), ('outc', 3, 0)],
-            (2, 6): [('quantc', 3, 0)],
-            (2, 7): [('quantc', 3, 1)],
+        steps = {
+            "cast_x": cast_x,
+            "turn_x": turn_x,
+            "scale_x": scale_x,
+            "quant_x": quant_x,
+            "first": first,
+            "square": square,
+            "rstd": rstd,
+            "norm": norm,
+            "turn_c": turn_c,
+            "copy_c": copy_c,
+            "quant_c": quant_c,
         }
-        for i in range(NT):
-            for k in range(NB):
-                b = nextbank()
-                mm2(i, k, b)
-                if pend:
-                    rope(*pend.pop())
-                pend.append((i, k, b))
-                for e in plan.get((i, k), []):
-                    do(*e)
-        rope(*pend.pop())
+        waiting = []
+        for i in range(TILES):
+            for k in range(GROUPS_B):
+                b = next_bank()
+                second(i, k, b)
+                if waiting:
+                    finish(*waiting.pop())
+                waiting.append((i, k, b))
+                for item in SCHEDULE.get((i, k), ()):
+                    steps[item[0]](*item[1:])
+        finish(*waiting.pop())

import math
from contextlib import ExitStack

import concourse.mybir as mybir
from concourse.masks import make_identity

TOKENS, DIM, QL, HEADS, HEAD = 512, 2048, 1536, 16, 256
NQ = HEADS * HEAD
HALF = 64
LOW = 32
POS0 = 37
EPS = 1e-6
FLOPS = 2 * TOKENS * DIM * QL + 2 * TOKENS * QL * NQ

F32 = mybir.dt.float32
BF16 = mybir.dt.bfloat16
I32 = mybir.dt.int32
U32 = mybir.dt.uint32
U8 = mybir.dt.uint8
F8 = mybir.dt.float8_e4m3fn
FP8X4 = mybir.dt.float8_e4m3fn_x4
FP4X4 = mybir.dt.float4_e2m1fn_x4
ALU = mybir.AluOpType
ACT = mybir.ActivationFunctionType

P = 128
TILES = TOKENS // P
PASSES_A = DIM // 512
PASSES_B = QL // 512
GROUPS_A = QL // 512
GROUPS_B = NQ // 512
WARM_UP = 5

RING = (0, 7, 3, 1, 2)
FIRST_BANKS = (6, 4, 5)

SCHEDULE = {
    (0, 0): (("cast_x", 3, 0), ("cast_x", 3, 1), ("scale_x", 2, 1), ("scale_x", 2, 2), ("scale_x", 2, 3), ("rstd", 1)),
    (0, 2): (("quant_x", 2, 0), ("quant_x", 2, 1)),
    (0, 3): (("norm", 1, 0), ("norm", 1, 1), ("norm", 1, 2)),
    (0, 5): (("turn_x", 3), ("turn_c", 1), ("copy_c", 1, 0), ("copy_c", 1, 1), ("first", 2, 0)),
    (0, 6): (
        ("scale_x", 3, 0),
        ("square", 2, 0),
        ("quant_c", 1, 0),
        ("quant_c", 1, 1),
        ("first", 2, 1),
        ("scale_x", 3, 1),
        ("square", 2, 1),
    ),
    (0, 7): (("first", 2, 2),),
    (1, 0): (("scale_x", 3, 2), ("scale_x", 3, 3), ("square", 2, 2), ("rstd", 2), ("quant_x", 3, 0)),
    (1, 1): (("norm", 2, 0), ("norm", 2, 1), ("norm", 2, 2)),
    (1, 4): (("turn_c", 2), ("copy_c", 2, 0), ("quant_x", 3, 1), ("copy_c", 2, 1)),
    (1, 6): (
        ("first", 3, 0),
        ("first", 3, 1),
        ("square", 3, 0),
        ("square", 3, 1),
        ("quant_c", 2, 0),
        ("quant_c", 2, 1),
        ("first", 3, 2),
    ),
    (1, 7): (("square", 3, 2), ("rstd", 3)),
    (2, 0): (("norm", 3, 0), ("norm", 3, 1), ("norm", 3, 2)),
    (2, 2): (("turn_c", 3), ("copy_c", 3, 0), ("copy_c", 3, 1)),
    (2, 4): (("quant_c", 3, 0), ("quant_c", 3, 1)),
}


def tile_mla_pa_w4_kernel(tc, x_bytes, x_scale, wq_a_words, wq_a_scales, q_norm_w, wq_b_words, wq_b_scales, out):
    nc = tc.nc
    x_rows = x_bytes.rearrange("b s k -> (b s) k")
    out_rows = out.rearrange("b s h d -> (b s) (h d)")

    with ExitStack() as ctx:
        keep = ctx.enter_context(tc.tile_pool(name="keep", bufs=1))
        work = ctx.enter_context(tc.tile_pool(name="work", bufs=3))
        psum = ctx.enter_context(tc.psum_pool(name="psum", bufs=1))
        ctx.enter_context(tc.manual_schedule())

        def bank(k):
            return psum.tile([P, 512], F32, name="bank%d" % k, tag="bank%d" % k)

        def kept(shape, dtype, name):
            return keep.tile(shape, dtype, name=name, align_bytes=256 if shape[-1] >= P else 64)

        x_raw = [kept([P, DIM], U8, "x_raw%d" % i) for i in range(TILES)]
        x_wide = [kept([P, DIM], BF16, "x_wide%d" % i) for i in range(TILES)]
        x_turned = [kept([P, PASSES_A, 512], BF16, "x_turned%d" % i) for i in range(TILES)]
        x_codes = [kept([P, PASSES_A, P], U32, "x_codes%d" % i) for i in range(TILES)]
        x_planes = [kept([P, PASSES_A, P], U8, "x_planes%d" % i) for i in range(TILES)]
        cn = [kept([P, QL], BF16, "cn%d" % i) for i in range(TILES)]
        c_turned = [kept([P, PASSES_B, 512], BF16, "c_turned%d" % i) for i in range(TILES)]
        c_codes = [kept([P, PASSES_B, P], U32, "c_codes%d" % i) for i in range(TILES)]
        c_planes = [kept([P, PASSES_B, P], U8, "c_planes%d" % i) for i in range(TILES)]
        parts = [kept([P, GROUPS_A], F32, "parts%d" % i) for i in range(TILES)]
        sums = [kept([P, 2], F32, "sums%d" % i) for i in range(TILES)]
        inv_rms = [kept([P, 1], F32, "inv_rms%d" % i) for i in range(TILES)]

        a_words = [kept([P, 2 * QL], U8, "a_words%d" % g) for g in range(PASSES_A)]
        a_planes = kept([P, PASSES_A, QL], U8, "a_planes")
        b_words = [[kept([P, NQ], U8, "b_words%d_%d" % (h, g)) for g in range(PASSES_B)] for h in range(2)]
        b_planes = [kept([P, PASSES_B, NQ // 2], U8, "b_planes%d" % h) for h in range(2)]
        scales = kept([P, PASSES_A, 4], F32, "scales")
        gain = kept([P, QL], BF16, "gain")

        gain_rows = kept([P, 512], BF16, "gain_rows")
        pick = kept([P, GROUPS_A], BF16, "pick")
        ident = kept([P, P], F32, "ident")
        zeros = kept([P, 512], BF16, "zeros")
        one = kept([P, 1], F32, "one")
        minus_half = kept([P, 1], F32, "minus_half")
        table_load = kept([P, 1], F32, "table_load")

        row = kept([P, HEADS], I32, "row")
        row_mod = kept([P, HEADS], I32, "row_mod")
        position = kept([P, HEADS], F32, "position")
        freq = kept([P, LOW], F32, "freq")
        turns = kept([P, HEADS, LOW], F32, "turns")
        whole = kept([P, HEADS, LOW], I32, "whole")
        angle = kept([P, 2, HEADS, LOW], F32, "angle")
        angle_abs = kept([P, HEADS, LOW], F32, "angle_abs")
        table = kept([P, 2, HEADS, 2, HALF], F32, "table")

        def load_x(i):
            nc.sync.dma_start(out=x_raw[i][:], in_=x_rows[P * i : P * (i + 1), :])

        def load_a_words(g):
            nc.sync.dma_start(out=a_words[g][:].bitcast(I32), in_=wq_a_words[g].bitcast(I32))

        def load_b_words(h):
            for g in range(PASSES_B):
                nc.sync.dma_start(out=b_words[h][g][:].bitcast(I32), in_=wq_b_words[g][:, NQ * h : NQ * (h + 1)].bitcast(I32))

        def zero_a_planes(g0, g1):
            nc.vector.memset(a_planes[:, g0:g1, :].rearrange("p g n -> p (g n)").bitcast(I32), 0)

        def load_a_planes(g0, g1):
            for q in range(4):
                nc.sync.dma_start(
                    out=a_planes[32 * q : 32 * q + 4, g0:g1, :].bitcast(I32),
                    in_=wq_a_scales[g0:g1, 4 * q : 4 * q + 4, :].rearrange("g r n -> r g n").bitcast(I32),
                )

        def zero_b_planes(h, g):
            nc.vector.memset(b_planes[h][:, g, :].bitcast(I32), 0)

        def load_b_planes(h):
            n0 = h * NQ // 2
            for q in range(4):
                nc.sync.dma_start(
                    out=b_planes[h][32 * q : 32 * q + 4, :, :].bitcast(I32),
                    in_=wq_b_scales[:, 4 * q : 4 * q + 4, n0 : n0 + NQ // 2].rearrange("g r n -> r g n").bitcast(I32),
                )

        def scale_freq(j0, j1, width):
            nc.vector.tensor_scalar(
                out=freq[:, j0:j1], in0=freq[:, 0:width], scalar1=10000.0 ** (-j0 / 64.0), scalar2=None, op0=ALU.mult
            )

        def spread(ap):
            return ap.rearrange("p h (a j) -> p a h j", a=2)

        def sine_tables():
            nc.scalar.activation(out=spread(table[:, 1, :, 0, :]), in_=angle[:], func=ACT.Sin, scale=2.0 * math.pi)
            nc.scalar.activation(out=angle_abs[:], in_=angle[:, 0, :, :], func=ACT.Abs)
            for a, size in ((0, angle_abs[:]), (1, angle[:, 1, :, :])):
                nc.scalar.activation(
                    out=table[:, 0, :, 0, LOW * a : LOW * (a + 1)],
                    in_=size,
                    func=ACT.Sin,
                    scale=-2.0 * math.pi,
                    bias=0.5 * math.pi,
                )

        def repeat_table(w):
            nc.gpsimd.tensor_scalar(
                out=table[:, w, :, 1, :], in0=table[:, w, :, 0, :], scalar1=1.0, scalar2=0.0, op0=ALU.mult, op1=ALU.add
            )

        x_banks = {}

        def widen_x(i, k0, k1):
            nc.scalar.copy(out=x_wide[i][:, k0:k1], in_=x_raw[i][:, k0:k1].bitcast(F8))

        def cast_x(i, part):
            widen_x(i, 1024 * part, 1024 * (part + 1))

        def turn_pass(i, g, b, slot):
            words = x_wide[i][:].bitcast(F32)
            for u in range(2):
                o = (2 * slot + u) * P
                nc.tensor.transpose(b[:, o : o + P], words[:, 256 * g + u : 256 * (g + 1) : 2], ident[:])

        def turn_x(i):
            x_banks[i] = [next_bank(), next_bank()]
            for g in range(PASSES_A):
                turn_pass(i, g, x_banks[i][g // 2], g % 2)

        def scale_pass(i, g, b, slot):
            nc.vector.tensor_tensor(
                out=x_turned[i][:, g, :].rearrange("p (r u e) -> p r u e", u=2, e=2),
                in0=b[:, 256 * slot : 256 * (slot + 1)].bitcast(BF16).rearrange("p (u r e) -> p r u e", u=2, e=2),
                in1=scales[:, g, :].rearrange("p (u e) -> p u e", e=2).unsqueeze(1).to_broadcast([P, P, 2, 2]),
                op=ALU.mult,
            )

        def scale_x(i, g):
            scale_pass(i, g, x_banks[i][g // 2], g % 2)

        def quantize(codes, planes, values, g0, g1):
            nc.vector.quantize_mx(
                out=codes[:, g0:g1, :].rearrange("p g r -> p (g r)").bitcast(FP8X4),
                scales=planes[:, g0:g1, :].rearrange("p g r -> p (g r)"),
                in_=values[:, g0:g1, :].rearrange("p g c -> p (g c)"),
            )

        def quantize_x(i, g0, g1):
            quantize(x_codes[i], x_planes[i], x_turned[i], g0, g1)

        def quant_x(i, part):
            quantize_x(i, 2 * part, 2 * part + 2)

        c_banks = {}

        def first_pass(i, g, n, b):
            nc.tensor.matmul_mx(
                out=b[:],
                lhsT=x_codes[i][:, g, :].bitcast(FP8X4),
                lhsT_scale=x_planes[i][:, g, :],
                rhs=a_words[g][:, 1024 * n : 1024 * (n + 1)].bitcast(FP4X4),
                rhs_scale=a_planes[:, g, 512 * n : 512 * (n + 1)],
                start=(g == 0),
                stop=(g == PASSES_A - 1),
            )

        def first(i, n):
            b = bank(FIRST_BANKS[n])
            c_banks.setdefault(i, []).append(b)
            for g in range(PASSES_A):
                first_pass(i, g, n, b)

        def square(i, n):
            junk = work.tile([P, 512], BF16, name="junk")
            nc.scalar.activation(
                out=junk[:], in_=c_banks[i][n][:], func=ACT.Square, scale=QL**-0.5, accum_out=parts[i][:, n : n + 1]
            )

        def add_parts(i):
            nc.vector.scalar_tensor_tensor(
                out=sums[i][:, 0:1], in0=parts[i][:, 0:1], scalar=EPS, in1=parts[i][:, 1:2], op0=ALU.add, op1=ALU.add
            )

        def invert(i):
            nc.vector.tensor_tensor(out=sums[i][:, 1:2], in0=sums[i][:, 0:1], in1=parts[i][:, 2:3], op=ALU.add)
            nc.gpsimd.tensor_tensor(out=inv_rms[i][:], in0=sums[i][:, 1:2], in1=minus_half[:], op=ALU.pow)

        def rstd(i):
            add_parts(i)
            invert(i)

        def norm(i, n):
            for u in range(2):
                cols = slice(512 * n + 256 * u, 512 * n + 256 * (u + 1))
                nc.vector.scalar_tensor_tensor(
                    out=cn[i][:, cols].rearrange("p (m e) -> p m e", e=2),
                    in0=c_banks[i][n][:].rearrange("p (m u e) -> p u m e", u=2, e=2)[:, u, :, :],
                    scalar=inv_rms[i][:],
                    in1=gain[:, cols].rearrange("p (m e) -> p m e", e=2),
                    op0=ALU.mult,
                    op1=ALU.mult,
                )

        cn_banks = {}

        def turn_cn_pass(i, g, b, slot):
            words = cn[i][:].bitcast(F32)
            for u in range(2):
                o = (2 * slot + u) * P
                nc.tensor.transpose(b[:, o : o + P], words[:, 256 * g + P * u : 256 * g + P * (u + 1)], ident[:])

        def copy_cn(i, g0, g1, b):
            nc.scalar.copy(
                out=c_turned[i][:, g0:g1, :].bitcast(F32).rearrange("p g (r u) -> p g r u", u=2),
                in_=b[:, 0 : 256 * (g1 - g0)].rearrange("p (g u r) -> p g r u", u=2, r=P),
            )

        def quantize_c(i, g0, g1):
            quantize(c_codes[i], c_planes[i], c_turned[i], g0, g1)

        def turn_c(i):
            cn_banks[i] = [bank(FIRST_BANKS[1]), bank(FIRST_BANKS[2])]
            for g in range(PASSES_B):
                turn_cn_pass(i, g, cn_banks[i][g // 2], g % 2)

        def copy_c(i, part):
            copy_cn(i, 2 * part, min(2 * part + 2, PASSES_B), cn_banks[i][part])

        def quant_c(i, part):
            quantize_c(i, 2 * part, min(2 * part + 2, PASSES_B))

        def second(i, k, b):
            h, kk = divmod(k, GROUPS_B // 2)
            for g in range(PASSES_B):
                nc.tensor.matmul_mx(
                    out=b[:],
                    lhsT=c_codes[i][:, g, :].bitcast(FP8X4),
                    lhsT_scale=c_planes[i][:, g, :],
                    rhs=b_words[h][g][:, 1024 * kk : 1024 * (kk + 1)].bitcast(FP4X4),
                    rhs_scale=b_planes[h][:, g, 512 * kk : 512 * (kk + 1)],
                    start=(g == 0),
                    stop=(g == PASSES_B - 1),
                )

        pair = {}

        def finish(i, k, b):
            s = k % 2
            if s == 0:
                pair["result"] = work.tile([P, 4, 2, 2, HALF], F32, name="result", bufs=8)
                pair["terms"] = work.tile([P, 4, 2, 2, HALF], F32, name="terms", bufs=4)
            result, terms = pair["result"], pair["terms"]
            alone = i == TILES - 1 and k >= GROUPS_B - 2
            heads = slice(2 * s, 2 * s + 2)
            halves = b[:].rearrange("p (h x c) -> p h x c", h=2, x=2)

            nc.vector.tensor_tensor(
                out=terms[:, heads, :, :, :].rearrange("p h w f j -> p w h (f j)"),
                in0=halves[:, :, 1, :].unsqueeze(1).to_broadcast([P, 2, 2, 2 * HALF]),
                in1=table[:, :, 2 * k : 2 * k + 2, :, :].rearrange("p w h f j -> p w h (f j)"),
                op=ALU.mult,
            )
            nc.scalar.copy(out=result[:, heads, 0, :, :].rearrange("p h f j -> p h (f j)"), in_=halves[:, :, 0, :])
            if s == 1 or alone:
                done = heads if alone else slice(0, 4)
                engine = nc.vector if alone and s == 1 else nc.gpsimd
                for f, op in ((0, ALU.subtract), (1, ALU.add)):
                    engine.tensor_tensor(
                        out=result[:, done, 1, f, :], in0=terms[:, done, 0, f, :], in1=terms[:, done, 1, 1 - f, :], op=op
                    )
                n0 = 512 * (k if alone else k - 1)
                nc.sync.dma_start(
                    out=out_rows[P * i : P * (i + 1), n0 : 512 * (k + 1)],
                    in_=result[:, done, :, :, :].rearrange("p h x f j -> p (h x f j)"),
                )

        nc.gpsimd.memset(zeros[:].bitcast(I32), 0)
        nc.gpsimd.iota(row[:], pattern=[[1, HEADS]], base=0, channel_multiplier=16)
        for m in range(WARM_UP):
            nc.tensor.matmul(bank(7)[:], zeros[:, 0:P], zeros[:], start=True, stop=True)
        nc.vector.memset(one[:], 1.0)
        nc.gpsimd.memset(gain_rows[:].bitcast(I32), 0)

        load_x(0)
        nc.sync.dma_start(out=scales[:], in_=x_scale.rearrange("a b (g p t) -> (a b p) g t", p=P, t=4))
        zero_a_planes(0, 2)
        load_a_planes(0, 2)
        load_a_words(0)
        load_x(1)
        nc.sync.dma_start(out=gain_rows[0:GROUPS_A, :], in_=q_norm_w.rearrange("(r c) -> r c", r=GROUPS_A))
        load_a_words(1)
        nc.vector.tensor_scalar(out=row_mod[:], in0=row[:], scalar1=255, scalar2=None, op0=ALU.bitwise_and)
        nc.vector.tensor_scalar(out=freq[:, 0:1], in0=one[:], scalar1=0.5 / math.pi, scalar2=None, op0=ALU.mult)
        zero_a_planes(2, 4)
        load_a_planes(2, 4)
        load_a_words(2)
        load_a_words(3)
        for m in (1, 2, 3):
            scale_freq(m, m + 1, 1)
        nc.vector.tensor_scalar(out=position[:], in0=row_mod[:], scalar1=float(POS0), scalar2=None, op0=ALU.add)
        zero_b_planes(0, 0)
        for m in (4, 8, 12):
            scale_freq(m, m + 4, 4)
        zero_b_planes(0, 1)
        scale_freq(16, 32, 16)
        nc.scalar.activation(out=table_load[:], in_=one[:], func=ACT.Sin)
        nc.vector.tensor_tensor(
            out=turns[:],
            in0=position[:].unsqueeze(2).to_broadcast([P, HEADS, LOW]),
            in1=freq[:].unsqueeze(1).to_broadcast([P, HEADS, LOW]),
            op=ALU.mult,
        )
        make_identity(nc, ident[:])
        nc.gpsimd.memset(minus_half[:], -0.5)
        nc.gpsimd.tensor_copy(out=pick[:], in_=ident[:, 0:GROUPS_A])

        c_banks[0] = [bank(n) for n in range(GROUPS_A)]
        x0_banks = [bank(3 + g) for g in range(PASSES_A)]
        for g in range(PASSES_A):
            widen_x(0, 512 * g, 512 * (g + 1))
        cast_x(1, 0)
        cast_x(1, 1)
        for g in range(PASSES_A):
            turn_pass(0, g, x0_banks[g], 0)

        scale_pass(0, 0, x0_banks[0], 0)
        zero_b_planes(0, 2)
        quantize_x(0, 0, 1)
        scale_pass(0, 1, x0_banks[1], 0)
        nc.vector.tensor_copy(out=whole[:], in_=turns[:])
        quantize_x(0, 1, 2)
        nc.vector.tensor_scalar(out=angle[:, 1, :, :], in0=turns[:], scalar1=0.01, scalar2=None, op0=ALU.mult)
        nc.vector.tensor_tensor(out=angle[:, 0, :, :], in0=turns[:], in1=whole[:], op=ALU.subtract)
        scale_pass(0, 2, x0_banks[2], 0)
        scale_pass(0, 3, x0_banks[3], 0)
        quantize_x(0, 2, 3)
        load_b_planes(0)
        load_x(2)
        load_b_words(0)
        load_x(3)
        load_b_words(1)
        zero_b_planes(1, 0)
        quantize_x(0, 3, 4)
        sine_tables()
        repeat_table(1)

        x_banks[1] = [bank(4), bank(5)]
        for g in range(2):
            for n in range(GROUPS_A):
                first_pass(0, g, n, c_banks[0][n])
        for g in range(PASSES_A):
            turn_pass(1, g, x_banks[1][g // 2], g % 2)
        for n in range(GROUPS_A):
            first_pass(0, 2, n, c_banks[0][n])
            first_pass(0, 3, n, c_banks[0][n])
            square(0, n)

        gain_bank, gain_bank_2 = bank(7), bank(3)
        for n, b, o in ((0, gain_bank, 0), (1, gain_bank, 512), (2, gain_bank_2, 0)):
            nc.tensor.matmul(
                b[:].bitcast(BF16)[:, o : o + 512],
                pick[:, n : n + 1].to_broadcast([P, P]),
                gain_rows[:].rearrange("p (m u e) -> p u m e", u=2, e=2),
                start=True,
                stop=True,
            )

        for g in range(3):
            scale_x(1, g)
        quant_x(1, 0)
        scale_x(1, 3)
        zero_b_planes(1, 1)
        quant_x(1, 1)
        nc.vector.tensor_copy(out=gain[:, 0:1024], in_=gain_bank[:].bitcast(BF16))
        nc.scalar.copy(out=gain[:, 1024:QL], in_=gain_bank_2[:, 0:256].bitcast(BF16))
        add_parts(0)
        zero_b_planes(1, 2)
        invert(0)
        load_b_planes(1)
        repeat_table(0)
        cast_x(2, 0)
        cast_x(2, 1)
        for n in range(GROUPS_A):
            norm(0, n)

        c_banks[1] = [bank(FIRST_BANKS[n]) for n in range(GROUPS_A)]
        for half in range(2):
            for n in range(GROUPS_A):
                first_pass(1, 2 * half, n, c_banks[1][n])
                first_pass(1, 2 * half + 1, n, c_banks[1][n])
        cn0_banks = [bank(k) for k in (0, 7, 3)]
        for g in range(PASSES_B):
            turn_cn_pass(0, g, cn0_banks[g], 0)
        x_banks[2] = [bank(1), bank(2)]
        for g in range(PASSES_A):
            turn_pass(2, g, x_banks[2][g // 2], g % 2)
        for g in range(PASSES_B):
            copy_cn(0, g, g + 1, cn0_banks[g])
            quantize_c(0, g, g + 1)
        scale_x(2, 0)
        for n in range(GROUPS_A):
            square(1, n)

        turn = [0]

        def next_bank():
            turn[0] += 1
            return bank(RING[(turn[0] - 1) % len(RING)])

        steps = {
            "cast_x": cast_x,
            "turn_x": turn_x,
            "scale_x": scale_x,
            "quant_x": quant_x,
            "first": first,
            "square": square,
            "rstd": rstd,
            "norm": norm,
            "turn_c": turn_c,
            "copy_c": copy_c,
            "quant_c": quant_c,
        }
        waiting = []
        for i in range(TILES):
            for k in range(GROUPS_B):
                b = next_bank()
                second(i, k, b)
                if waiting:
                    finish(*waiting.pop())
                waiting.append((i, k, b))
                for item in SCHEDULE.get((i, k), ()):
                    steps[item[0]](*item[1:])
        finish(*waiting.pop())
